import numpy as np
import ml_dtypes


def mxq(x, axis, fmt="e4m3"):
    dtype, down = {"e4m3": (ml_dtypes.float8_e4m3fn, 7), "e5m2": (ml_dtypes.float8_e5m2, 14)}[fmt]
    v = np.moveaxis(np.asarray(x, np.float32).astype(ml_dtypes.bfloat16).astype(np.float64), axis, -1)
    blocks = v.reshape(v.shape[:-1] + (-1, 32))
    amax = np.abs(blocks).max(-1, keepdims=True)
    byte = np.maximum(np.where(amax > 0, np.frexp(amax)[1] - 1 + 127, 0) - down, 1)
    scale = np.exp2(byte - 127.0)
    codes = (blocks / scale).astype(np.float32).astype(dtype).astype(np.float64)
    return np.moveaxis((codes * scale).reshape(v.shape), -1, axis)


WIDE = False


def mx_kscale(k):
    if not WIDE:
        return np.ones(k)
    levels = np.array([20, -20, 10, -10, 0])
    if k % 512:
        return np.exp2(np.random.permutation(np.resize(levels, k // 32))).repeat(32)
    a = np.empty((k // 512, 16))
    for p in range(k // 512):
        a[p, :8] = np.random.permutation(np.resize(levels, 8))
        for g in range(8):
            far = levels[np.abs(levels - a[p, g]) >= 10]
            a[p, g + 8] = far[np.random.randint(len(far))]
    return np.exp2(a.ravel()).repeat(32)


BF16 = ml_dtypes.bfloat16


def bf(x):
    return np.asarray(x, np.float32).astype(BF16)


def f64(x):
    return np.asarray(x).astype(np.float64)


B, I, O, G, P = 2048, 512, 512, 5, 3
GRID_RANGE = (-1.0, 1.0)
L = G + P


def make_grid():
    h = (GRID_RANGE[1] - GRID_RANGE[0]) / G
    n = G + 2 * P + 1
    return np.linspace(GRID_RANGE[0] - P * h, GRID_RANGE[1] + P * h, n)


def b_spline(x, grid, k):
    x = x[..., None]
    g = grid[None, None, :]
    basis = ((x >= g[..., :-1]) & (x < g[..., 1:])).astype(np.float64)
    for p in range(1, k + 1):
        left_denom = g[..., p:-1] - g[..., :-(p + 1)]
        right_denom = g[..., p + 1:] - g[..., 1:-p]
        left_denom = np.where(left_denom > 0, left_denom, np.ones_like(left_denom))
        right_denom = np.where(right_denom > 0, right_denom, np.ones_like(right_denom))
        left = (x - g[..., :-(p + 1)]) / left_denom * basis[..., :-1]
        right = (g[..., p + 1:] - x) / right_denom * basis[..., 1:]
        basis = left + right
    return basis


def d_b_spline(x, grid, k):
    low = b_spline(x, grid, k - 1)
    a = k / (grid[k:-1] - grid[:-(k + 1)])
    c = k / (grid[k + 1:] - grid[1:-k])
    return a * low[..., :-1] - c * low[..., 1:]


def setup_inputs():
    u = mx_kscale(O)
    x = np.random.uniform(-1.0, 1.0, (B, I))
    base_weight = np.random.uniform(-1.0, 1.0, (O, I)) * 3.0 / np.sqrt(I) / u[:, None]
    spline_weight = np.random.standard_normal((O, I, L)) * 1.5 / np.sqrt(I) / u[:, None, None]
    g = np.random.standard_normal((B, O)) * np.exp2(np.random.randint(-12, 1, (B, 1))) * 4.0 * u
    return {"x": bf(x), "base_weight": bf(base_weight), "spline_weight": bf(spline_weight), "grad_out": bf(g)}


def reference(x, base_weight, spline_weight, grad_out):
    x = f64(x)
    gq = mxq(f64(grad_out), 1, "e5m2")
    g_base = gq @ mxq(f64(base_weight), 0, "e4m3")
    g_basis = (gq @ mxq(f64(spline_weight).reshape(O, I * L), 0, "e4m3")).reshape(B, I, L)
    dbasis = d_b_spline(x, make_grid(), P)
    return g_base + (dbasis * g_basis).sum(axis=-1)

@@ -1,0 +1,322 @@
+from contextlib import ExitStack
+
+import concourse.mybir as mybir
+from concourse.masks import make_identity
+
+F32 = mybir.dt.float32
+BF16 = mybir.dt.bfloat16
+U32 = mybir.dt.uint32
+U8 = mybir.dt.uint8
+E4X4 = mybir.dt.float8_e4m3fn_x4
+E5X4 = mybir.dt.float8_e5m2_x4
+ALU = mybir.AluOpType
+ACT = mybir.ActivationFunctionType
+
+P = 128
+B, I, O, L = 2048, 512, 512, 8
+FLOPS = 2 * B * O * (I + I * L)
+
+H = 0.4
+XI = [-1.0 + H * k for k in range(6)]
+A = 1.25 ** 0.5
+S = A / H
+NTILES = 16
+NPLANES = 8
+LEAD = 6
+
+
+def tile_kanlayer_t_kernel(tc, x, base_weight, spline_weight, grad_out, out):
+    nc = tc.nc
+    with ExitStack() as ctx:
+        keep = ctx.enter_context(tc.tile_pool(name="keep", bufs=1))
+        grp = ctx.enter_context(tc.tile_pool(name="grp", bufs=2))
+        plp = ctx.enter_context(tc.tile_pool(name="plp", bufs=2))
+        fnp = ctx.enter_context(tc.tile_pool(name="fnp", bufs=3))
+        fbp = ctx.enter_context(tc.tile_pool(name="fbp", bufs=2))
+        outp = ctx.enter_context(tc.tile_pool(name="outp", bufs=3))
+        psum = ctx.enter_context(tc.psum_pool(name="psum", bufs=LEAD))
+        aux = ctx.enter_context(tc.psum_pool(name="aux", bufs=2))
+        ctx.enter_context(tc.manual_schedule())
+
+        ident = keep.tile([P, P], F32)
+        make_identity(nc, ident[:])
+        ident_bf = keep.tile([P, P], BF16)
+        make_identity(nc, ident_bf[:])
+        w_codes = keep.tile([P, 4, L, P], U32, align_bytes=64)
+        w_scales = keep.tile([P, 4, L, P], U8, align_bytes=64)
+        wb_codes = keep.tile([P, I], U32, align_bytes=64)
+        wb_scales = keep.tile([P, I], U8, align_bytes=64)
+        g_codes = keep.tile([P, 2, B], U32, align_bytes=64)
+        g_scales = keep.tile([P, 2, B], U8, align_bytes=64)
+        xT = keep.tile([P, 4, B], BF16)
+        x_sb = keep.tile([P, 16, I], BF16)
+        g_sb = keep.tile([P, 16, O], BF16)
+        w_raw = keep.tile([P, 4, 4, L * P], BF16)
+        wb_raw = keep.tile([P, 4, I], BF16)
+        wg = keep.tile([P, L, P, 4], BF16, align_bytes=64)
+
+        g_view = grad_out.rearrange("(n p) o -> p n o", p=P)
+        x_view = x.rearrange("(n p) i -> p n i", p=P)
+        sw = spline_weight.rearrange("o i l -> o (i l)")
+
+        def load_g(bc):
+            nc.sync.dma_start(out=g_sb[:, 4 * bc : 4 * bc + 4, :], in_=g_view[:, 4 * bc : 4 * bc + 4, :])
+
+        def load_x(bc):
+            nc.sync.dma_start(out=x_sb[:, 4 * bc : 4 * bc + 4, :], in_=x_view[:, 4 * bc : 4 * bc + 4, :])
+
+        def load_w(j):
+            nc.sync.dma_start(
+                out=w_raw[:, j], in_=sw[:, L * P * j : L * P * (j + 1)].rearrange("(q t) c -> q t c", t=4)
+            )
+
+        load_x(0)
+        load_g(0)
+        load_w(0)
+        load_g(1)
+        load_x(1)
+        nc.sync.dma_start(out=wb_raw[:], in_=base_weight.rearrange("(q t) c -> q t c", t=4))
+        for bc in range(2, 4):
+            load_g(bc)
+            load_x(bc)
+        for j in range(1, 4):
+            load_w(j)
+
+        ggs = {}
+        xts = {}
+        xps = {}
+
+        def g_transpose(bc, c2):
+            xt = aux.tile([P, 2, 2, P], F32, tag="aux", name="xt")
+            xts[(bc, c2)] = xt
+            for n2 in range(2):
+                gw = g_sb[:, 4 * bc + 2 * c2 + n2, :].bitcast(F32)
+                for u in range(2):
+                    nc.tensor.transpose(xt[:, n2, u, :], gw[:, u : 2 * P : 2], ident[:])
+
+        def g_copy(bc, c2, on_vector):
+            if c2 == 0:
+                ggs[bc] = grp.tile([P, 512, 4], BF16, align_bytes=64, tag="gg", name="gg")
+            ggf = ggs[bc][:].rearrange("p b t -> p (b t)").bitcast(F32).rearrange("p (b u) -> p b u", u=2)
+            dst = ggf[:, 256 * c2 : 256 * c2 + 256, :].rearrange("p (n b) u -> p n b u", n=2)
+            src = xts[(bc, c2)][:].rearrange("p n u b -> p n b u")
+            if on_vector:
+                nc.vector.tensor_copy(out=dst, in_=src)
+            else:
+                nc.scalar.copy(out=dst, in_=src)
+
+        def g_quantise(bc):
+            gg2 = grp.tile([P, 512, 4], BF16, align_bytes=64, tag="gg2", name="gg2")
+            flat = ggs[bc][:].rearrange("p b t -> p (b t)")
+            flat2 = gg2[:].rearrange("p b t -> p (b t)")
+            nc.vector.tensor_scalar(out=flat2, in0=flat, scalar1=-2.0, scalar2=None, op0=ALU.mult)
+            cols = slice(512 * bc, 512 * bc + 512)
+            nc.vector.quantize_mx(out=g_codes[:, 0, cols].bitcast(E5X4), scales=g_scales[:, 0, cols], in_=flat)
+            nc.vector.quantize_mx(out=g_codes[:, 1, cols].bitcast(E5X4), scales=g_scales[:, 1, cols], in_=flat2)
+
+        def x_transpose(bc, j2):
+            xp = aux.tile([P, 2, 512], BF16, tag="aux", name="xp")
+            xps[(bc, j2)] = xp
+            for jj in range(2):
+                j = 2 * j2 + jj
+                for q in range(4):
+                    nc.tensor.transpose(
+                        xp[:, jj, P * q : P * q + P], x_sb[:, 4 * bc + q, P * j : P * j + P], ident_bf[:]
+                    )
+
+        def x_copy(bc, j2):
+            nc.scalar.copy(out=xT[:, 2 * j2 : 2 * j2 + 2, 512 * bc : 512 * bc + 512], in_=xps[(bc, j2)][:])
+
+        def w_regroup(j, on_vector):
+            src = w_raw[:, j].rearrange("p t (i l) -> p l i t", l=L)
+            cut = 4 if j == 0 else 2
+            if on_vector:
+                nc.vector.tensor_copy(out=wg[:, 0:cut], in_=src[:, 0:cut])
+            else:
+                nc.scalar.copy(out=wg[:, cut:L], in_=src[:, cut:L])
+
+        def w_quantise(j):
+            nc.vector.quantize_mx(
+                out=w_codes[:, j].rearrange("p l i -> p (l i)").bitcast(E4X4),
+                scales=w_scales[:, j].rearrange("p l i -> p (l i)"),
+                in_=wg[:].rearrange("p l i t -> p (l i t)"),
+            )
+
+        def pre_base():
+            wbg = grp.tile([P, 512, 4], BF16, align_bytes=64, tag="gg", name="wbg")
+            nc.scalar.copy(out=wbg[:], in_=wb_raw[:].rearrange("p t i -> p i t"))
+            nc.vector.quantize_mx(
+                out=wb_codes[:].bitcast(E4X4), scales=wb_scales[:], in_=wbg[:].rearrange("p i t -> p (i t)")
+            )
+
+        fns = {}
+        fbs = {}
+        pls = {}
+        banks = {}
+        obs = {}
+
+        def func_v(t):
+            j, bc = t // 4, t % 4
+            xs = xT[:, j, 512 * bc : 512 * bc + 512]
+            pl = plp.tile([P, 5, 512], F32, name="pl")
+            pls[t] = pl
+            for k in range(1, 4):
+                nc.vector.tensor_scalar(
+                    out=pl[:, k, :], in0=xs, scalar1=XI[k], scalar2=XI[k + 1], op0=ALU.max, op1=ALU.min
+                )
+
+        def func_s_head(t):
+            j, bc = t // 4, t % 4
+            xs = xT[:, j, 512 * bc : 512 * bc + 512]
+            pl = pls[t]
+            fn = fnp.tile([P, 6, 512], F32, name="fn")
+            fb = fbp.tile([P, 4, 512], F32, name="fb")
+            fns[t] = fn
+            fbs[t] = fb
+            nc.scalar.activation(out=pl[:, 0, :], in_=xs, func=ACT.Relu, scale=-1.0 / H, bias=XI[1] / H)
+            nc.scalar.activation(out=pl[:, 4, :], in_=xs, func=ACT.Relu, scale=1.0 / H, bias=-XI[4] / H)
+            nc.scalar.activation(out=fn[:, 0, :], in_=pl[:, 0, :], func=ACT.Square, scale=A, bias=0.0)
+            nc.scalar.activation(out=fn[:, 1, :], in_=pl[:, 0, :], func=ACT.Square, scale=-A, bias=A)
+            nc.scalar.activation(out=fn[:, 5, :], in_=pl[:, 4, :], func=ACT.Square, scale=A, bias=0.0)
+            nc.scalar.activation(out=fb[:, 3, :], in_=pl[:, 4, :], func=ACT.Square, scale=-A, bias=A)
+
+        def func_s_tail(t):
+            pl, fn, fb = pls[t], fns[t], fbs[t]
+            for k in range(1, 4):
+                nc.scalar.activation(out=fn[:, k + 1, :], in_=pl[:, k, :], func=ACT.Square, scale=S, bias=-S * XI[k])
+                nc.scalar.activation(out=fb[:, k - 1, :], in_=pl[:, k, :], func=ACT.Square, scale=-S, bias=S * XI[k + 1])
+
+        def mx(bank, j, bc, v, l, start, stop):
+            gc = slice(512 * bc, 512 * bc + 512)
+            if l < L:
+                lhsT, lhsT_scale = w_codes[:, j, l, :], w_scales[:, j, l, :]
+            else:
+                lhsT, lhsT_scale = wb_codes[:, P * j : P * j + P], wb_scales[:, P * j : P * j + P]
+            nc.tensor.matmul_mx(
+                out=bank[:],
+                lhsT=lhsT.bitcast(E4X4),
+                lhsT_scale=lhsT_scale,
+                rhs=g_codes[:, v, gc].bitcast(E5X4),
+                rhs_scale=g_scales[:, v, gc],
+                start=start,
+                stop=stop,
+            )
+
+        def issue_mx(q):
+            t, p = q // NPLANES, q % NPLANES
+            j, bc = t // 4, t % 4
+            bank = psum.tile([P, 512], F32, tag="mx", name="bank")
+            banks[q] = bank
+            if p == 4:
+                mx(bank, j, bc, 0, 2, True, False)
+                mx(bank, j, bc, 0, 2, False, False)
+                mx(bank, j, bc, 1, 0, False, True)
+            elif p == 7:
+                mx(bank, j, bc, 0, L, True, True)
+            else:
+                m = p if p < 4 else p - 1
+                mx(bank, j, bc, 0, m + 2, True, False)
+                mx(bank, j, bc, 1, m + 1, False, False)
+                mx(bank, j, bc, 0, m, False, True)
+
+        def consume(q):
+            t, p = q // NPLANES, q % NPLANES
+            fn = fns[t]
+            bank = banks[q]
+            if p == 0:
+                nc.vector.scalar_tensor_tensor(
+                    out=fn[:, 0, :], in0=fn[:, 0, :], scalar=-1.25, in1=bank[:], op0=ALU.add, op1=ALU.mult
+                )
+            elif p < 4 or p == 5:
+                a = p if p < 4 else 4
+                nc.vector.scalar_tensor_tensor(
+                    out=fn[:, a, :], in0=fn[:, a, :], scalar=1.25, in1=bank[:], op0=ALU.add, op1=ALU.mult
+                )
+            elif p == 6:
+                nc.vector.tensor_tensor(out=fn[:, 5, :], in0=fn[:, 5, :], in1=bank[:], op=ALU.mult)
+            elif p == 4:
+                nc.vector.scalar_tensor_tensor(
+                    out=fn[:, 0, :], in0=bank[:], scalar=0.625, in1=fn[:, 0, :], op0=ALU.mult, op1=ALU.subtract
+                )
+                nc.vector.tensor_tensor(out=fn[:, 0:2, :], in0=fn[:, 0:2, :], in1=fn[:, 2:4, :], op=ALU.add)
+            else:
+                nc.vector.tensor_tensor(out=fn[:, 4, :], in0=fn[:, 4, :], in1=bank[:], op=ALU.add)
+
+        def adder(t):
+            fn = fns[t]
+            ob = aux.tile([P, 4, P], F32, tag="aux", name="ob")
+            obs[t] = ob
+            for r in range(4):
+                for a in (0, 1, 4, 5):
+                    nc.tensor.matmul(
+                        out=ob[:, r, :],
+                        lhsT=fn[:, a, P * r : P * r + P],
+                        rhs=ident[:],
+                        is_transpose=True,
+                        start=(a == 0),
+                        stop=(a == 5),
+                    )
+
+        def finish(t):
+            j, bc = t // 4, t % 4
+            ot = outp.tile([P, 4, P], F32, name="ot")
+            nc.scalar.copy(out=ot[:], in_=obs[t][:])
+            nc.sync.dma_start(
+                out=out[512 * bc : 512 * bc + 512, P * j : P * j + P].rearrange("(r p) i -> p r i", p=P), in_=ot[:]
+            )
+
+        x_transpose(0, 0)
+        x_copy(0, 0)
+        g_transpose(0, 0)
+        g_transpose(0, 1)
+        g_copy(0, 0, False)
+        g_copy(0, 1, False)
+        func_v(0)
+        func_s_head(0)
+        g_quantise(0)
+        w_regroup(0, True)
+        w_regroup(0, False)
+        x_transpose(1, 0)
+        g_transpose(1, 0)
+        g_copy(1, 0, True)
+        g_transpose(1, 1)
+        g_copy(1, 1, True)
+        w_quantise(0)
+        func_s_tail(0)
+        x_copy(1, 0)
+        for q in range(LEAD):
+            issue_mx(q)
+        g_quantise(1)
+        pre_base()
+        for t in range(NTILES):
+            if t + 1 < NTILES:
+                func_v(t + 1)
+                func_s_head(t + 1)
+                func_s_tail(t + 1)
+            if t >= 1:
+                finish(t - 1)
+            if t + 2 < 4:
+                x_transpose(t + 2, 0)
+                g_transpose(t + 2, 0)
+                x_copy(t + 2, 0)
+                g_transpose(t + 2, 1)
+                g_copy(t + 2, 0, False)
+                g_copy(t + 2, 1, False)
+            if 2 <= t < 6:
+                x_transpose(t - 2, 1)
+                x_copy(t - 2, 1)
+            if t % 4 == 1 and t // 4 + 1 < 4:
+                w_regroup(t // 4 + 1, False)
+            if 2 <= t + 1 < 4:
+                g_quantise(t + 1)
+            if t % 4 == 2 and t // 4 + 1 < 4:
+                w_regroup(t // 4 + 1, True)
+                w_quantise(t // 4 + 1)
+            nc.vector.tensor_tensor(out=fns[t][:, 1:5, :], in0=fns[t][:, 1:5, :], in1=fbs[t][:], op=ALU.subtract)
+            for p in range(NPLANES):
+                q = NPLANES * t + p
+                consume(q)
+                if q + LEAD < NPLANES * NTILES:
+                    issue_mx(q + LEAD)
+            adder(t)
+        finish(NTILES - 1)

@@ -18,11 +18,12 @@ FLOPS = 2 * B * O * (I + I * L)
 
 H = 0.4
 XI = [-1.0 + H * k for k in range(6)]
-A = 1.25 ** 0.5
-S = A / H
+S = 2.5 ** 0.5 / H
 NTILES = 16
-NPLANES = 8
 LEAD = 6
+ADD = [None, 2.5, 1.5, -0.5, -2.5, None]
+PLANES = [0, 1, 2, 3, 4, 5, "c"]
+NPLANES = len(PLANES)
 
 
 def tile_kanlayer_t_kernel(tc, x, base_weight, spline_weight, grad_out, out):
@@ -109,7 +110,7 @@ def tile_kanlayer_t_kernel(tc, x, base_weight, spline_weight, grad_out, out):
             gg2 = grp.tile([P, 512, 4], BF16, align_bytes=64, tag="gg2", name="gg2")
             flat = ggs[bc][:].rearrange("p b t -> p (b t)")
             flat2 = gg2[:].rearrange("p b t -> p (b t)")
-            nc.vector.tensor_scalar(out=flat2, in0=flat, scalar1=-2.0, scalar2=None, op0=ALU.mult)
+            nc.vector.tensor_scalar(out=flat2, in0=flat, scalar1=-0.5, scalar2=None, op0=ALU.mult)
             cols = slice(512 * bc, 512 * bc + 512)
             nc.vector.quantize_mx(out=g_codes[:, 0, cols].bitcast(E5X4), scales=g_scales[:, 0, cols], in_=flat)
             nc.vector.quantize_mx(out=g_codes[:, 1, cols].bitcast(E5X4), scales=g_scales[:, 1, cols], in_=flat2)
@@ -160,31 +161,23 @@ def tile_kanlayer_t_kernel(tc, x, base_weight, spline_weight, grad_out, out):
             xs = xT[:, j, 512 * bc : 512 * bc + 512]
             pl = plp.tile([P, 5, 512], F32, name="pl")
             pls[t] = pl
+            nc.vector.tensor_scalar(out=pl[:, 0, :], in0=xs, scalar1=XI[1], scalar2=None, op0=ALU.min)
             for k in range(1, 4):
                 nc.vector.tensor_scalar(
                     out=pl[:, k, :], in0=xs, scalar1=XI[k], scalar2=XI[k + 1], op0=ALU.max, op1=ALU.min
                 )
+            nc.vector.tensor_scalar(out=pl[:, 4, :], in0=xs, scalar1=XI[4], scalar2=None, op0=ALU.max)
 
-        def func_s_head(t):
-            j, bc = t // 4, t % 4
-            xs = xT[:, j, 512 * bc : 512 * bc + 512]
+        def func_s(t):
             pl = pls[t]
             fn = fnp.tile([P, 6, 512], F32, name="fn")
             fb = fbp.tile([P, 4, 512], F32, name="fb")
             fns[t] = fn
             fbs[t] = fb
-            nc.scalar.activation(out=pl[:, 0, :], in_=xs, func=ACT.Relu, scale=-1.0 / H, bias=XI[1] / H)
-            nc.scalar.activation(out=pl[:, 4, :], in_=xs, func=ACT.Relu, scale=1.0 / H, bias=-XI[4] / H)
-            nc.scalar.activation(out=fn[:, 0, :], in_=pl[:, 0, :], func=ACT.Square, scale=A, bias=0.0)
-            nc.scalar.activation(out=fn[:, 1, :], in_=pl[:, 0, :], func=ACT.Square, scale=-A, bias=A)
-            nc.scalar.activation(out=fn[:, 5, :], in_=pl[:, 4, :], func=ACT.Square, scale=A, bias=0.0)
-            nc.scalar.activation(out=fb[:, 3, :], in_=pl[:, 4, :], func=ACT.Square, scale=-A, bias=A)
-
-        def func_s_tail(t):
-            pl, fn, fb = pls[t], fns[t], fbs[t]
-            for k in range(1, 4):
-                nc.scalar.activation(out=fn[:, k + 1, :], in_=pl[:, k, :], func=ACT.Square, scale=S, bias=-S * XI[k])
-                nc.scalar.activation(out=fb[:, k - 1, :], in_=pl[:, k, :], func=ACT.Square, scale=-S, bias=S * XI[k + 1])
+            for k in range(5):
+                nc.scalar.activation(out=fn[:, k, :], in_=pl[:, k, :], func=ACT.Square, scale=-S, bias=S * XI[k + 1])
+                rise = fb[:, k, :] if k < 4 else fn[:, 5, :]
+                nc.scalar.activation(out=rise, in_=pl[:, k, :], func=ACT.Square, scale=S, bias=-S * XI[k])
 
         def mx(bank, j, bc, v, l, start, stop):
             gc = slice(512 * bc, 512 * bc + 512)
@@ -203,44 +196,38 @@ def tile_kanlayer_t_kernel(tc, x, base_weight, spline_weight, grad_out, out):
             )
 
         def issue_mx(q):
-            t, p = q // NPLANES, q % NPLANES
+            t, p = q // NPLANES, PLANES[q % NPLANES]
             j, bc = t // 4, t % 4
             bank = psum.tile([P, 512], F32, tag="mx", name="bank")
             banks[q] = bank
-            if p == 4:
-                mx(bank, j, bc, 0, 2, True, False)
-                mx(bank, j, bc, 0, 2, False, False)
-                mx(bank, j, bc, 1, 0, False, True)
-            elif p == 7:
-                mx(bank, j, bc, 0, L, True, True)
+            if p == "c":
+                mx(bank, j, bc, 0, L, True, False)
+                mx(bank, j, bc, 0, 5, False, False)
+                mx(bank, j, bc, 1, 3, False, False)
+                mx(bank, j, bc, 1, 2, False, True)
             else:
-                m = p if p < 4 else p - 1
-                mx(bank, j, bc, 0, m + 2, True, False)
-                mx(bank, j, bc, 1, m + 1, False, False)
-                mx(bank, j, bc, 0, m, False, True)
+                mx(bank, j, bc, 0, p + 1, True, False)
+                mx(bank, j, bc, 1, p, False, False)
+                mx(bank, j, bc, 1, p + 2, False, True)
 
         def consume(q):
-            t, p = q // NPLANES, q % NPLANES
+            t, p = q // NPLANES, PLANES[q % NPLANES]
             fn = fns[t]
             bank = banks[q]
-            if p == 0:
+            if p == "c":
+                nc.vector.tensor_tensor(out=fn[:, 5, :], in0=fn[:, 5, :], in1=bank[:], op=ALU.add)
+            elif p == 0:
+                nc.vector.tensor_tensor(out=fn[:, 0, :], in0=fn[:, 0, :], in1=bank[:], op=ALU.mult)
+            elif p == 5:
                 nc.vector.scalar_tensor_tensor(
-                    out=fn[:, 0, :], in0=fn[:, 0, :], scalar=-1.25, in1=bank[:], op0=ALU.add, op1=ALU.mult
+                    out=fn[:, 5, :], in0=fn[:, 5, :], scalar=-1.0, in1=bank[:], op0=ALU.mult, op1=ALU.mult
                 )
-            elif p < 4 or p == 5:
-                a = p if p < 4 else 4
-                nc.vector.scalar_tensor_tensor(
-                    out=fn[:, a, :], in0=fn[:, a, :], scalar=1.25, in1=bank[:], op0=ALU.add, op1=ALU.mult
-                )
-            elif p == 6:
-                nc.vector.tensor_tensor(out=fn[:, 5, :], in0=fn[:, 5, :], in1=bank[:], op=ALU.mult)
-            elif p == 4:
-                nc.vector.scalar_tensor_tensor(
-                    out=fn[:, 0, :], in0=bank[:], scalar=0.625, in1=fn[:, 0, :], op0=ALU.mult, op1=ALU.subtract
-                )
-                nc.vector.tensor_tensor(out=fn[:, 0:2, :], in0=fn[:, 0:2, :], in1=fn[:, 2:4, :], op=ALU.add)
             else:
-                nc.vector.tensor_tensor(out=fn[:, 4, :], in0=fn[:, 4, :], in1=bank[:], op=ALU.add)
+                nc.vector.scalar_tensor_tensor(
+                    out=fn[:, p, :], in0=fn[:, p, :], scalar=ADD[p], in1=bank[:], op0=ALU.add, op1=ALU.mult
+                )
+            if p == 4:
+                nc.vector.tensor_tensor(out=fn[:, 0:2, :], in0=fn[:, 0:2, :], in1=fn[:, 2:4, :], op=ALU.add)
 
         def adder(t):
             fn = fns[t]
@@ -272,7 +259,6 @@ def tile_kanlayer_t_kernel(tc, x, base_weight, spline_weight, grad_out, out):
         g_copy(0, 0, False)
         g_copy(0, 1, False)
         func_v(0)
-        func_s_head(0)
         g_quantise(0)
         w_regroup(0, True)
         w_regroup(0, False)
@@ -282,7 +268,7 @@ def tile_kanlayer_t_kernel(tc, x, base_weight, spline_weight, grad_out, out):
         g_transpose(1, 1)
         g_copy(1, 1, True)
         w_quantise(0)
-        func_s_tail(0)
+        func_s(0)
         x_copy(1, 0)
         for q in range(LEAD):
             issue_mx(q)
@@ -291,8 +277,7 @@ def tile_kanlayer_t_kernel(tc, x, base_weight, spline_weight, grad_out, out):
         for t in range(NTILES):
             if t + 1 < NTILES:
                 func_v(t + 1)
-                func_s_head(t + 1)
-                func_s_tail(t + 1)
+                func_s(t + 1)
             if t >= 1:
                 finish(t - 1)
             if t + 2 < 4:

@@ -19,6 +19,7 @@ FLOPS = 2 * B * O * (I + I * L)
 H = 0.4
 XI = [-1.0 + H * k for k in range(6)]
 S = 2.5 ** 0.5 / H
+Q = 6.25
 NTILES = 16
 LEAD = 6
 ADD = [None, 2.5, 1.5, -0.5, -2.5, None]
@@ -31,9 +32,9 @@ def tile_kanlayer_t_kernel(tc, x, base_weight, spline_weight, grad_out, out):
     with ExitStack() as ctx:
         keep = ctx.enter_context(tc.tile_pool(name="keep", bufs=1))
         grp = ctx.enter_context(tc.tile_pool(name="grp", bufs=2))
-        plp = ctx.enter_context(tc.tile_pool(name="plp", bufs=2))
+        clp = ctx.enter_context(tc.tile_pool(name="clp", bufs=2))
+        ap = ctx.enter_context(tc.tile_pool(name="ap", bufs=2))
         fnp = ctx.enter_context(tc.tile_pool(name="fnp", bufs=3))
-        fbp = ctx.enter_context(tc.tile_pool(name="fbp", bufs=2))
         outp = ctx.enter_context(tc.tile_pool(name="outp", bufs=3))
         psum = ctx.enter_context(tc.psum_pool(name="psum", bufs=LEAD))
         aux = ctx.enter_context(tc.psum_pool(name="aux", bufs=2))
@@ -54,7 +55,6 @@ def tile_kanlayer_t_kernel(tc, x, base_weight, spline_weight, grad_out, out):
         g_sb = keep.tile([P, 16, O], BF16)
         w_raw = keep.tile([P, 4, 4, L * P], BF16)
         wb_raw = keep.tile([P, 4, I], BF16)
-        wg = keep.tile([P, L, P, 4], BF16, align_bytes=64)
 
         g_view = grad_out.rearrange("(n p) o -> p n o", p=P)
         x_view = x.rearrange("(n p) i -> p n i", p=P)
@@ -77,15 +77,18 @@ def tile_kanlayer_t_kernel(tc, x, base_weight, spline_weight, grad_out, out):
         load_g(1)
         load_x(1)
         nc.sync.dma_start(out=wb_raw[:], in_=base_weight.rearrange("(q t) c -> q t c", t=4))
-        for bc in range(2, 4):
-            load_g(bc)
-            load_x(bc)
-        for j in range(1, 4):
-            load_w(j)
+        load_g(2)
+        load_x(2)
+        load_w(1)
+        load_g(3)
+        load_x(3)
+        load_w(2)
+        load_w(3)
 
         ggs = {}
         xts = {}
         xps = {}
+        wgs = {}
 
         def g_transpose(bc, c2):
             xt = aux.tile([P, 2, 2, P], F32, tag="aux", name="xt")
@@ -128,56 +131,82 @@ def tile_kanlayer_t_kernel(tc, x, base_weight, spline_weight, grad_out, out):
         def x_copy(bc, j2):
             nc.scalar.copy(out=xT[:, 2 * j2 : 2 * j2 + 2, 512 * bc : 512 * bc + 512], in_=xps[(bc, j2)][:])
 
-        def w_regroup(j, on_vector):
-            src = w_raw[:, j].rearrange("p t (i l) -> p l i t", l=L)
-            cut = 4 if j == 0 else 2
-            if on_vector:
-                nc.vector.tensor_copy(out=wg[:, 0:cut], in_=src[:, 0:cut])
-            else:
-                nc.scalar.copy(out=wg[:, cut:L], in_=src[:, cut:L])
+        def w_regroup(j, h, engines):
+            wg = grp.tile([P, 4, P, 4], BF16, align_bytes=64, tag="wg", name="wg")
+            wgs[(j, h)] = wg
+            src = w_raw[:, j].rearrange("p t (i l) -> p i l t", l=L)
+            dst = wg[:].rearrange("p l i t -> p i l t")
+            l0 = 0
+            for name, n in engines:
+                s, d = src[:, :, 4 * h + l0 : 4 * h + l0 + n, :], dst[:, :, l0 : l0 + n, :]
+                if name == "v":
+                    nc.vector.tensor_copy(out=d, in_=s)
+                elif name == "s":
+                    nc.scalar.copy(out=d, in_=s)
+                else:
+                    nc.gpsimd.tensor_scalar(out=d, in0=s, scalar1=1.0, scalar2=0.0, op0=ALU.mult, op1=ALU.add)
+                l0 += n
 
-        def w_quantise(j):
+        def w_quantise(j, h):
             nc.vector.quantize_mx(
-                out=w_codes[:, j].rearrange("p l i -> p (l i)").bitcast(E4X4),
-                scales=w_scales[:, j].rearrange("p l i -> p (l i)"),
-                in_=wg[:].rearrange("p l i t -> p (l i t)"),
+                out=w_codes[:, j, 4 * h : 4 * h + 4].rearrange("p l i -> p (l i)").bitcast(E4X4),
+                scales=w_scales[:, j, 4 * h : 4 * h + 4].rearrange("p l i -> p (l i)"),
+                in_=wgs[(j, h)][:].rearrange("p l i t -> p (l i t)"),
             )
 
-        def pre_base():
+        def base_regroup():
             wbg = grp.tile([P, 512, 4], BF16, align_bytes=64, tag="gg", name="wbg")
+            wgs["b"] = wbg
             nc.scalar.copy(out=wbg[:], in_=wb_raw[:].rearrange("p t i -> p i t"))
+
+        def base_quantise():
             nc.vector.quantize_mx(
-                out=wb_codes[:].bitcast(E4X4), scales=wb_scales[:], in_=wbg[:].rearrange("p i t -> p (i t)")
+                out=wb_codes[:].bitcast(E4X4), scales=wb_scales[:], in_=wgs["b"][:].rearrange("p i t -> p (i t)")
             )
 
+        cls = {}
+        avs = {}
         fns = {}
-        fbs = {}
-        pls = {}
         banks = {}
         obs = {}
 
-        def func_v(t):
+        def xs_of(t):
             j, bc = t // 4, t % 4
-            xs = xT[:, j, 512 * bc : 512 * bc + 512]
-            pl = plp.tile([P, 5, 512], F32, name="pl")
-            pls[t] = pl
-            nc.vector.tensor_scalar(out=pl[:, 0, :], in0=xs, scalar1=XI[1], scalar2=None, op0=ALU.min)
-            for k in range(1, 4):
-                nc.vector.tensor_scalar(
-                    out=pl[:, k, :], in0=xs, scalar1=XI[k], scalar2=XI[k + 1], op0=ALU.max, op1=ALU.min
-                )
-            nc.vector.tensor_scalar(out=pl[:, 4, :], in0=xs, scalar1=XI[4], scalar2=None, op0=ALU.max)
+            return xT[:, j, 512 * bc : 512 * bc + 512]
+
+        def clamps(t):
+            xs = xs_of(t)
+            cl = clp.tile([P, 5, 512], F32, name="cl")
+            cls[t] = cl
+            ts = nc.vector.tensor_scalar
+            for k in (1, 2, 3):
+                ts(out=cl[:, k, :], in0=xs, scalar1=XI[k], scalar2=XI[k + 1], op0=ALU.max, op1=ALU.min)
+            ts(out=cl[:, 0, :], in0=xs, scalar1=XI[1], scalar2=H, op0=ALU.subtract, op1=ALU.min)
+            ts(out=cl[:, 4, :], in0=xs, scalar1=XI[4], scalar2=-H, op0=ALU.subtract, op1=ALU.max)
 
         def func_s(t):
-            pl = pls[t]
+            xs = xs_of(t)
+            cl = cls[t]
+            av = ap.tile([P, 4, 512], F32, name="av")
             fn = fnp.tile([P, 6, 512], F32, name="fn")
-            fb = fbp.tile([P, 4, 512], F32, name="fb")
-            fns[t] = fn
-            fbs[t] = fb
-            for k in range(5):
-                nc.scalar.activation(out=fn[:, k, :], in_=pl[:, k, :], func=ACT.Square, scale=-S, bias=S * XI[k + 1])
-                rise = fb[:, k, :] if k < 4 else fn[:, 5, :]
-                nc.scalar.activation(out=rise, in_=pl[:, k, :], func=ACT.Square, scale=S, bias=-S * XI[k])
+            avs[t], fns[t] = av, fn
+            act = nc.scalar.activation
+            for k in (2, 3):
+                act(out=av[:, k, :], in_=cl[:, k - 1, :], func=ACT.Square, scale=S, bias=-S * XI[k - 1])
+                act(out=fn[:, k, :], in_=cl[:, k, :], func=ACT.Square, scale=-S, bias=S * XI[k + 1])
+                nc.gpsimd.tensor_tensor(out=fn[:, k, :], in0=fn[:, k, :], in1=av[:, k, :], op=ALU.subtract)
+            act(out=av[:, 0, :], in_=cl[:, 0, :], func=ACT.Abs, scale=Q / H, bias=0.0)
+            act(out=av[:, 1, :], in_=cl[:, 4, :], func=ACT.Abs, scale=Q / H, bias=0.0)
+            act(out=fn[:, 0, :], in_=xs, func=ACT.Relu, scale=-S, bias=S * XI[1])
+            act(out=fn[:, 5, :], in_=xs, func=ACT.Relu, scale=S, bias=-S * XI[4])
+            act(out=fn[:, 0, :], in_=fn[:, 0, :], func=ACT.Square, scale=1.0, bias=0.0)
+            act(out=fn[:, 5, :], in_=fn[:, 5, :], func=ACT.Square, scale=1.0, bias=0.0)
+
+        def func_v(t):
+            cl, av, fn = cls[t], avs[t], fns[t]
+            stt = nc.vector.scalar_tensor_tensor
+            stt(out=fn[:, 1, :], in0=av[:, 0, :], scalar=-2.0 * Q, in1=cl[:, 0, :], op0=ALU.add, op1=ALU.mult)
+            stt(out=fn[:, 4, :], in0=av[:, 1, :], scalar=-2.0 * Q, in1=cl[:, 4, :], op0=ALU.add, op1=ALU.mult)
 
         def mx(bank, j, bc, v, l, start, stop):
             gc = slice(512 * bc, 512 * bc + 512)
@@ -226,8 +255,10 @@ def tile_kanlayer_t_kernel(tc, x, base_weight, spline_weight, grad_out, out):
                 nc.vector.scalar_tensor_tensor(
                     out=fn[:, p, :], in0=fn[:, p, :], scalar=ADD[p], in1=bank[:], op0=ALU.add, op1=ALU.mult
                 )
-            if p == 4:
-                nc.vector.tensor_tensor(out=fn[:, 0:2, :], in0=fn[:, 0:2, :], in1=fn[:, 2:4, :], op=ALU.add)
+
+        def pair_add(t):
+            fn = fns[t]
+            nc.vector.tensor_tensor(out=fn[:, 0:2, :], in0=fn[:, 0:2, :], in1=fn[:, 2:4, :], op=ALU.add)
 
         def adder(t):
             fn = fns[t]
@@ -255,53 +286,65 @@ def tile_kanlayer_t_kernel(tc, x, base_weight, spline_weight, grad_out, out):
         x_transpose(0, 0)
         x_copy(0, 0)
         g_transpose(0, 0)
+        clamps(0)
+        g_copy(0, 0, True)
         g_transpose(0, 1)
-        g_copy(0, 0, False)
         g_copy(0, 1, False)
-        func_v(0)
         g_quantise(0)
-        w_regroup(0, True)
-        w_regroup(0, False)
+        w_regroup(0, 0, [("v", 1), ("s", 1), ("g", 2)])
+        w_regroup(0, 1, [("v", 2), ("g", 2)])
+        w_quantise(0, 0)
+        func_s(0)
         x_transpose(1, 0)
         g_transpose(1, 0)
         g_copy(1, 0, True)
         g_transpose(1, 1)
-        g_copy(1, 1, True)
-        w_quantise(0)
-        func_s(0)
         x_copy(1, 0)
+        w_quantise(0, 1)
+        g_copy(1, 1, False)
         for q in range(LEAD):
             issue_mx(q)
+        clamps(1)
+        func_v(0)
+        base_regroup()
         g_quantise(1)
-        pre_base()
         for t in range(NTILES):
-            if t + 1 < NTILES:
-                func_v(t + 1)
-                func_s(t + 1)
-            if t >= 1:
-                finish(t - 1)
-            if t + 2 < 4:
+            if t == 0:
+                base_quantise()
+            if t < 2:
                 x_transpose(t + 2, 0)
                 g_transpose(t + 2, 0)
                 x_copy(t + 2, 0)
                 g_transpose(t + 2, 1)
                 g_copy(t + 2, 0, False)
                 g_copy(t + 2, 1, False)
-            if 2 <= t < 6:
+            elif t < 6:
                 x_transpose(t - 2, 1)
                 x_copy(t - 2, 1)
-            if t % 4 == 1 and t // 4 + 1 < 4:
-                w_regroup(t // 4 + 1, False)
-            if 2 <= t + 1 < 4:
+            if t + 1 < NTILES:
+                func_s(t + 1)
+            if t in (1, 2):
                 g_quantise(t + 1)
-            if t % 4 == 2 and t // 4 + 1 < 4:
-                w_regroup(t // 4 + 1, True)
-                w_quantise(t // 4 + 1)
-            nc.vector.tensor_tensor(out=fns[t][:, 1:5, :], in0=fns[t][:, 1:5, :], in1=fbs[t][:], op=ALU.subtract)
+            jn = t // 4 + 1
+            if jn < 4:
+                if t % 4 == 1:
+                    w_regroup(jn, 0, [("g", 4)])
+                if t % 4 == 2:
+                    w_quantise(jn, 0)
+                    w_regroup(jn, 1, [("g", 4)])
+                if t % 4 == 3:
+                    w_quantise(jn, 1)
             for p in range(NPLANES):
                 q = NPLANES * t + p
                 consume(q)
+                if p == 1 and t >= 1:
+                    finish(t - 1)
                 if q + LEAD < NPLANES * NTILES:
                     issue_mx(q + LEAD)
+            pair_add(t)
             adder(t)
+            if t + 2 < NTILES:
+                clamps(t + 2)
+            if t + 1 < NTILES:
+                func_v(t + 1)
         finish(NTILES - 1)

@@ -22,7 +22,7 @@ S = 2.5 ** 0.5 / H
 Q = 6.25
 NTILES = 16
 LEAD = 6
-ADD = [None, 2.5, 1.5, -0.5, -2.5, None]
+ADD = [None, 1.5, 0.5, -0.5, -1.5, None]
 PLANES = [0, 1, 2, 3, 4, 5, "c"]
 NPLANES = len(PLANES)
 
@@ -44,8 +44,8 @@ def tile_kanlayer_t_kernel(tc, x, base_weight, spline_weight, grad_out, out):
         make_identity(nc, ident[:])
         ident_bf = keep.tile([P, P], BF16)
         make_identity(nc, ident_bf[:])
-        w_codes = keep.tile([P, 4, L, P], U32, align_bytes=64)
-        w_scales = keep.tile([P, 4, L, P], U8, align_bytes=64)
+        w_codes = keep.tile([P, 4, L + 1, P], U32, align_bytes=64)
+        w_scales = keep.tile([P, 4, L + 1, P], U8, align_bytes=64)
         wb_codes = keep.tile([P, I], U32, align_bytes=64)
         wb_scales = keep.tile([P, I], U8, align_bytes=64)
         g_codes = keep.tile([P, 2, B], U32, align_bytes=64)
@@ -147,6 +147,19 @@ def tile_kanlayer_t_kernel(tc, x, base_weight, spline_weight, grad_out, out):
                     nc.gpsimd.tensor_scalar(out=d, in0=s, scalar1=1.0, scalar2=0.0, op0=ALU.mult, op1=ALU.add)
                 l0 += n
 
+        def w_negate(j):
+            wn = grp.tile([P, P, 4], BF16, align_bytes=64, tag="wn", name="wn")
+            wgs[(j, "n")] = wn
+            src = w_raw[:, j].rearrange("p t (i l) -> p i l t", l=L)[:, :, 6, :]
+            nc.gpsimd.tensor_scalar(out=wn[:], in0=src, scalar1=-1.0, scalar2=0.0, op0=ALU.mult, op1=ALU.add)
+
+        def w_quantise_negated(j):
+            nc.vector.quantize_mx(
+                out=w_codes[:, j, L].bitcast(E4X4),
+                scales=w_scales[:, j, L],
+                in_=wgs[(j, "n")][:].rearrange("p i t -> p (i t)"),
+            )
+
         def w_quantise(j, h):
             nc.vector.quantize_mx(
                 out=w_codes[:, j, 4 * h : 4 * h + 4].rearrange("p l i -> p (l i)").bitcast(E4X4),
@@ -210,7 +223,7 @@ def tile_kanlayer_t_kernel(tc, x, base_weight, spline_weight, grad_out, out):
 
         def mx(bank, j, bc, v, l, start, stop):
             gc = slice(512 * bc, 512 * bc + 512)
-            if l < L:
+            if l <= L:
                 lhsT, lhsT_scale = w_codes[:, j, l, :], w_scales[:, j, l, :]
             else:
                 lhsT, lhsT_scale = wb_codes[:, P * j : P * j + P], wb_scales[:, P * j : P * j + P]
@@ -230,10 +243,9 @@ def tile_kanlayer_t_kernel(tc, x, base_weight, spline_weight, grad_out, out):
             bank = psum.tile([P, 512], F32, tag="mx", name="bank")
             banks[q] = bank
             if p == "c":
-                mx(bank, j, bc, 0, L, True, False)
-                mx(bank, j, bc, 0, 5, False, False)
-                mx(bank, j, bc, 1, 3, False, False)
-                mx(bank, j, bc, 1, 2, False, True)
+                mx(bank, j, bc, 0, L + 1, True, False)
+                mx(bank, j, bc, 1, L, False, False)
+                mx(bank, j, bc, 1, 1, False, True)
             else:
                 mx(bank, j, bc, 0, p + 1, True, False)
                 mx(bank, j, bc, 1, p, False, False)
@@ -256,23 +268,23 @@ def tile_kanlayer_t_kernel(tc, x, base_weight, spline_weight, grad_out, out):
                     out=fn[:, p, :], in0=fn[:, p, :], scalar=ADD[p], in1=bank[:], op0=ALU.add, op1=ALU.mult
                 )
 
-        def pair_add(t):
+        def plane_add(t):
             fn = fns[t]
-            nc.vector.tensor_tensor(out=fn[:, 0:2, :], in0=fn[:, 0:2, :], in1=fn[:, 2:4, :], op=ALU.add)
+            nc.vector.tensor_tensor(out=fn[:, 0:3, :], in0=fn[:, 0:3, :], in1=fn[:, 3:6, :], op=ALU.add)
 
         def adder(t):
             fn = fns[t]
             ob = aux.tile([P, 4, P], F32, tag="aux", name="ob")
             obs[t] = ob
             for r in range(4):
-                for a in (0, 1, 4, 5):
+                for a in range(3):
                     nc.tensor.matmul(
                         out=ob[:, r, :],
                         lhsT=fn[:, a, P * r : P * r + P],
                         rhs=ident[:],
                         is_transpose=True,
                         start=(a == 0),
-                        stop=(a == 5),
+                        stop=(a == 2),
                     )
 
         def finish(t):
@@ -293,6 +305,7 @@ def tile_kanlayer_t_kernel(tc, x, base_weight, spline_weight, grad_out, out):
         g_quantise(0)
         w_regroup(0, 0, [("v", 1), ("s", 1), ("g", 2)])
         w_regroup(0, 1, [("v", 2), ("g", 2)])
+        w_negate(0)
         w_quantise(0, 0)
         func_s(0)
         x_transpose(1, 0)
@@ -301,6 +314,7 @@ def tile_kanlayer_t_kernel(tc, x, base_weight, spline_weight, grad_out, out):
         g_transpose(1, 1)
         x_copy(1, 0)
         w_quantise(0, 1)
+        w_quantise_negated(0)
         g_copy(1, 1, False)
         for q in range(LEAD):
             issue_mx(q)
@@ -332,8 +346,10 @@ def tile_kanlayer_t_kernel(tc, x, base_weight, spline_weight, grad_out, out):
                 if t % 4 == 2:
                     w_quantise(jn, 0)
                     w_regroup(jn, 1, [("g", 4)])
+                    w_negate(jn)
                 if t % 4 == 3:
                     w_quantise(jn, 1)
+                    w_quantise_negated(jn)
             for p in range(NPLANES):
                 q = NPLANES * t + p
                 consume(q)
@@ -341,10 +357,10 @@ def tile_kanlayer_t_kernel(tc, x, base_weight, spline_weight, grad_out, out):
                     finish(t - 1)
                 if q + LEAD < NPLANES * NTILES:
                     issue_mx(q + LEAD)
-            pair_add(t)
-            adder(t)
             if t + 2 < NTILES:
                 clamps(t + 2)
+            plane_add(t)
+            adder(t)
             if t + 1 < NTILES:
                 func_v(t + 1)
         finish(NTILES - 1)

@@ -33,7 +33,7 @@ def tile_kanlayer_t_kernel(tc, x, base_weight, spline_weight, grad_out, out):
         keep = ctx.enter_context(tc.tile_pool(name="keep", bufs=1))
         grp = ctx.enter_context(tc.tile_pool(name="grp", bufs=2))
         clp = ctx.enter_context(tc.tile_pool(name="clp", bufs=2))
-        ap = ctx.enter_context(tc.tile_pool(name="ap", bufs=2))
+        avp = ctx.enter_context(tc.tile_pool(name="avp", bufs=2))
         fnp = ctx.enter_context(tc.tile_pool(name="fnp", bufs=3))
         outp = ctx.enter_context(tc.tile_pool(name="outp", bufs=3))
         psum = ctx.enter_context(tc.psum_pool(name="psum", bufs=LEAD))
@@ -52,7 +52,6 @@ def tile_kanlayer_t_kernel(tc, x, base_weight, spline_weight, grad_out, out):
         g_scales = keep.tile([P, 2, B], U8, align_bytes=64)
         xT = keep.tile([P, 4, B], BF16)
         x_sb = keep.tile([P, 16, I], BF16)
-        g_sb = keep.tile([P, 16, O], BF16)
         w_raw = keep.tile([P, 4, 4, L * P], BF16)
         wb_raw = keep.tile([P, 4, I], BF16)
 
@@ -60,8 +59,12 @@ def tile_kanlayer_t_kernel(tc, x, base_weight, spline_weight, grad_out, out):
         x_view = x.rearrange("(n p) i -> p n i", p=P)
         sw = spline_weight.rearrange("o i l -> o (i l)")
 
+        g_sbs = {}
+
         def load_g(bc):
-            nc.sync.dma_start(out=g_sb[:, 4 * bc : 4 * bc + 4, :], in_=g_view[:, 4 * bc : 4 * bc + 4, :])
+            g_sb = grp.tile([P, 4, O], BF16, tag="g_sb", name="g_sb")
+            g_sbs[bc] = g_sb
+            nc.sync.dma_start(out=g_sb[:], in_=g_view[:, 4 * bc : 4 * bc + 4, :])
 
         def load_x(bc):
             nc.sync.dma_start(out=x_sb[:, 4 * bc : 4 * bc + 4, :], in_=x_view[:, 4 * bc : 4 * bc + 4, :])
@@ -74,16 +77,12 @@ def tile_kanlayer_t_kernel(tc, x, base_weight, spline_weight, grad_out, out):
         load_x(0)
         load_g(0)
         load_w(0)
-        load_g(1)
         load_x(1)
+        load_g(1)
         nc.sync.dma_start(out=wb_raw[:], in_=base_weight.rearrange("(q t) c -> q t c", t=4))
-        load_g(2)
         load_x(2)
         load_w(1)
-        load_g(3)
         load_x(3)
-        load_w(2)
-        load_w(3)
 
         ggs = {}
         xts = {}
@@ -94,7 +93,7 @@ def tile_kanlayer_t_kernel(tc, x, base_weight, spline_weight, grad_out, out):
             xt = aux.tile([P, 2, 2, P], F32, tag="aux", name="xt")
             xts[(bc, c2)] = xt
             for n2 in range(2):
-                gw = g_sb[:, 4 * bc + 2 * c2 + n2, :].bitcast(F32)
+                gw = g_sbs[bc][:, 2 * c2 + n2, :].bitcast(F32)
                 for u in range(2):
                     nc.tensor.transpose(xt[:, n2, u, :], gw[:, u : 2 * P : 2], ident[:])
 
@@ -118,57 +117,48 @@ def tile_kanlayer_t_kernel(tc, x, base_weight, spline_weight, grad_out, out):
             nc.vector.quantize_mx(out=g_codes[:, 0, cols].bitcast(E5X4), scales=g_scales[:, 0, cols], in_=flat)
             nc.vector.quantize_mx(out=g_codes[:, 1, cols].bitcast(E5X4), scales=g_scales[:, 1, cols], in_=flat2)
 
-        def x_transpose(bc, j2):
-            xp = aux.tile([P, 2, 512], BF16, tag="aux", name="xp")
-            xps[(bc, j2)] = xp
-            for jj in range(2):
-                j = 2 * j2 + jj
-                for q in range(4):
-                    nc.tensor.transpose(
-                        xp[:, jj, P * q : P * q + P], x_sb[:, 4 * bc + q, P * j : P * j + P], ident_bf[:]
-                    )
+        def x_transpose(t):
+            j, bc = t // 4, t % 4
+            xp = aux.tile([P, 512], BF16, tag="aux", name="xp")
+            xps[t] = xp
+            for r in range(4):
+                nc.tensor.transpose(xp[:, P * r : P * r + P], x_sb[:, 4 * bc + r, P * j : P * j + P], ident_bf[:])
 
-        def x_copy(bc, j2):
-            nc.scalar.copy(out=xT[:, 2 * j2 : 2 * j2 + 2, 512 * bc : 512 * bc + 512], in_=xps[(bc, j2)][:])
+        def x_copy(t):
+            j, bc = t // 4, t % 4
+            nc.scalar.copy(out=xT[:, j, 512 * bc : 512 * bc + 512], in_=xps[t][:])
 
-        def w_regroup(j, h, engines):
-            wg = grp.tile([P, 4, P, 4], BF16, align_bytes=64, tag="wg", name="wg")
-            wgs[(j, h)] = wg
+        def w_regroup(j, c, engines):
+            wg = grp.tile([P, 3, P, 4], BF16, align_bytes=64, tag="wg", name="wg")
+            wgs[(j, c)] = wg
             src = w_raw[:, j].rearrange("p t (i l) -> p i l t", l=L)
             dst = wg[:].rearrange("p l i t -> p i l t")
-            l0 = 0
+            k = 0
             for name, n in engines:
-                s, d = src[:, :, 4 * h + l0 : 4 * h + l0 + n, :], dst[:, :, l0 : l0 + n, :]
+                l0 = 3 * c + k
+                d = dst[:, :, k : k + n, :]
+                s = src[:, :, l0 : l0 + n, :] if l0 < L else src[:, :, 6:7, :]
                 if name == "v":
                     nc.vector.tensor_copy(out=d, in_=s)
                 elif name == "s":
                     nc.scalar.copy(out=d, in_=s)
-                else:
+                elif name == "g":
                     nc.gpsimd.tensor_scalar(out=d, in0=s, scalar1=1.0, scalar2=0.0, op0=ALU.mult, op1=ALU.add)
-                l0 += n
+                else:
+                    nc.gpsimd.tensor_scalar(out=d, in0=s, scalar1=-1.0, scalar2=0.0, op0=ALU.mult, op1=ALU.add)
+                k += n
 
-        def w_negate(j):
-            wn = grp.tile([P, P, 4], BF16, align_bytes=64, tag="wn", name="wn")
-            wgs[(j, "n")] = wn
-            src = w_raw[:, j].rearrange("p t (i l) -> p i l t", l=L)[:, :, 6, :]
-            nc.gpsimd.tensor_scalar(out=wn[:], in0=src, scalar1=-1.0, scalar2=0.0, op0=ALU.mult, op1=ALU.add)
-
-        def w_quantise_negated(j):
-            nc.vector.quantize_mx(
-                out=w_codes[:, j, L].bitcast(E4X4),
-                scales=w_scales[:, j, L],
-                in_=wgs[(j, "n")][:].rearrange("p i t -> p (i t)"),
-            )
-
-        def w_quantise(j, h):
-            nc.vector.quantize_mx(
-                out=w_codes[:, j, 4 * h : 4 * h + 4].rearrange("p l i -> p (l i)").bitcast(E4X4),
-                scales=w_scales[:, j, 4 * h : 4 * h + 4].rearrange("p l i -> p (l i)"),
-                in_=wgs[(j, h)][:].rearrange("p l i t -> p (l i t)"),
-            )
+        def w_quantise(j, c):
+            for k, n in ((0, 2), (2, 1)):
+                cols = slice(3 * c + k, 3 * c + k + n)
+                nc.vector.quantize_mx(
+                    out=w_codes[:, j, cols].rearrange("p l i -> p (l i)").bitcast(E4X4),
+                    scales=w_scales[:, j, cols].rearrange("p l i -> p (l i)"),
+                    in_=wgs[(j, c)][:, k : k + n].rearrange("p l i t -> p (l i t)"),
+                )
 
         def base_regroup():
-            wbg = grp.tile([P, 512, 4], BF16, align_bytes=64, tag="gg", name="wbg")
+            wbg = keep.tile([P, 512, 4], BF16, align_bytes=64, name="wbg")
             wgs["b"] = wbg
             nc.scalar.copy(out=wbg[:], in_=wb_raw[:].rearrange("p t i -> p i t"))
 
@@ -178,6 +168,7 @@ def tile_kanlayer_t_kernel(tc, x, base_weight, spline_weight, grad_out, out):
             )
 
         cls = {}
+        zts = {}
         avs = {}
         fns = {}
         banks = {}
@@ -189,37 +180,45 @@ def tile_kanlayer_t_kernel(tc, x, base_weight, spline_weight, grad_out, out):
 
         def clamps(t):
             xs = xs_of(t)
-            cl = clp.tile([P, 5, 512], F32, name="cl")
-            cls[t] = cl
+            zt = clp.tile([P, 4, 512], F32, name="zt")
+            cl = clp.tile([P, 2, 512], F32, name="cl")
+            zts[t], cls[t] = zt, cl
             ts = nc.vector.tensor_scalar
-            for k in (1, 2, 3):
-                ts(out=cl[:, k, :], in0=xs, scalar1=XI[k], scalar2=XI[k + 1], op0=ALU.max, op1=ALU.min)
-            ts(out=cl[:, 0, :], in0=xs, scalar1=XI[1], scalar2=H, op0=ALU.subtract, op1=ALU.min)
-            ts(out=cl[:, 4, :], in0=xs, scalar1=XI[4], scalar2=-H, op0=ALU.subtract, op1=ALU.max)
-
-        def func_s(t):
-            xs = xs_of(t)
-            cl = cls[t]
-            av = ap.tile([P, 4, 512], F32, name="av")
-            fn = fnp.tile([P, 6, 512], F32, name="fn")
-            avs[t], fns[t] = av, fn
-            act = nc.scalar.activation
+            ts(out=zt[:, 0, :], in0=xs, scalar1=XI[1], scalar2=H, op0=ALU.subtract, op1=ALU.min)
+            ts(out=zt[:, 3, :], in0=xs, scalar1=XI[4], scalar2=-H, op0=ALU.subtract, op1=ALU.max)
             for k in (2, 3):
-                act(out=av[:, k, :], in_=cl[:, k - 1, :], func=ACT.Square, scale=S, bias=-S * XI[k - 1])
-                act(out=fn[:, k, :], in_=cl[:, k, :], func=ACT.Square, scale=-S, bias=S * XI[k + 1])
-                nc.gpsimd.tensor_tensor(out=fn[:, k, :], in0=fn[:, k, :], in1=av[:, k, :], op=ALU.subtract)
-            act(out=av[:, 0, :], in_=cl[:, 0, :], func=ACT.Abs, scale=Q / H, bias=0.0)
-            act(out=av[:, 1, :], in_=cl[:, 4, :], func=ACT.Abs, scale=Q / H, bias=0.0)
-            act(out=fn[:, 0, :], in_=xs, func=ACT.Relu, scale=-S, bias=S * XI[1])
-            act(out=fn[:, 5, :], in_=xs, func=ACT.Relu, scale=S, bias=-S * XI[4])
-            act(out=fn[:, 0, :], in_=fn[:, 0, :], func=ACT.Square, scale=1.0, bias=0.0)
-            act(out=fn[:, 5, :], in_=fn[:, 5, :], func=ACT.Square, scale=1.0, bias=0.0)
+                ts(out=cl[:, k - 2, :], in0=xs, scalar1=XI[k - 1], scalar2=XI[k + 1], op0=ALU.max, op1=ALU.min)
 
-        def func_v(t):
-            cl, av, fn = cls[t], avs[t], fns[t]
-            stt = nc.vector.scalar_tensor_tensor
-            stt(out=fn[:, 1, :], in0=av[:, 0, :], scalar=-2.0 * Q, in1=cl[:, 0, :], op0=ALU.add, op1=ALU.mult)
-            stt(out=fn[:, 4, :], in0=av[:, 1, :], scalar=-2.0 * Q, in1=cl[:, 4, :], op0=ALU.add, op1=ALU.mult)
+        def func_s(t, part):
+            xs = xs_of(t)
+            cl, zt = cls[t], zts[t]
+            act = nc.scalar.activation
+            if part == 0:
+                avs[t] = avp.tile([P, 4, 512], F32, name="av")
+                fns[t] = fnp.tile([P, 7, 512], F32, name="fn")
+            av, fn = avs[t], fns[t]
+            if part == 0:
+                act(out=fn[:, 0, :], in_=xs, func=ACT.Relu, scale=-S, bias=S * XI[1])
+                act(out=fn[:, 5, :], in_=xs, func=ACT.Relu, scale=S, bias=-S * XI[4])
+                act(out=fn[:, 0, :], in_=fn[:, 0, :], func=ACT.Square, scale=1.0, bias=0.0)
+                act(out=fn[:, 5, :], in_=fn[:, 5, :], func=ACT.Square, scale=1.0, bias=0.0)
+            elif part == 1:
+                act(out=av[:, 0, :], in_=zt[:, 0, :], func=ACT.Abs, scale=Q / H, bias=0.0)
+                act(out=av[:, 3, :], in_=zt[:, 3, :], func=ACT.Abs, scale=Q / H, bias=0.0)
+            else:
+                k = part
+                act(out=av[:, k - 1, :], in_=cl[:, k - 2, :], func=ACT.Abs, scale=Q / H, bias=-Q * XI[k] / H)
+                act(out=zt[:, k - 1, :], in_=cl[:, k - 2, :], func=ACT.Identity, scale=1.0, bias=-XI[k])
+
+        def func_v(t, a, b):
+            nc.vector.scalar_tensor_tensor(
+                out=fns[t][:, a:b, :],
+                in0=avs[t][:, a - 1 : b - 1, :],
+                scalar=-2.0 * Q,
+                in1=zts[t][:, a - 1 : b - 1, :],
+                op0=ALU.add,
+                op1=ALU.mult,
+            )
 
         def mx(bank, j, bc, v, l, start, stop):
             gc = slice(512 * bc, 512 * bc + 512)
@@ -256,7 +255,7 @@ def tile_kanlayer_t_kernel(tc, x, base_weight, spline_weight, grad_out, out):
             fn = fns[t]
             bank = banks[q]
             if p == "c":
-                nc.vector.tensor_tensor(out=fn[:, 5, :], in0=fn[:, 5, :], in1=bank[:], op=ALU.add)
+                nc.scalar.copy(out=fn[:, 6, :], in_=bank[:])
             elif p == 0:
                 nc.vector.tensor_tensor(out=fn[:, 0, :], in0=fn[:, 0, :], in1=bank[:], op=ALU.mult)
             elif p == 5:
@@ -270,21 +269,21 @@ def tile_kanlayer_t_kernel(tc, x, base_weight, spline_weight, grad_out, out):
 
         def plane_add(t):
             fn = fns[t]
-            nc.vector.tensor_tensor(out=fn[:, 0:3, :], in0=fn[:, 0:3, :], in1=fn[:, 3:6, :], op=ALU.add)
+            nc.vector.tensor_tensor(out=fn[:, 0, :], in0=fn[:, 0, :], in1=fn[:, 1, :], op=ALU.add)
 
         def adder(t):
             fn = fns[t]
             ob = aux.tile([P, 4, P], F32, tag="aux", name="ob")
             obs[t] = ob
             for r in range(4):
-                for a in range(3):
+                for a in (0, 2, 3, 4, 5, 6):
                     nc.tensor.matmul(
                         out=ob[:, r, :],
                         lhsT=fn[:, a, P * r : P * r + P],
                         rhs=ident[:],
                         is_transpose=True,
                         start=(a == 0),
-                        stop=(a == 2),
+                        stop=(a == 6),
                     )
 
         def finish(t):
@@ -295,72 +294,85 @@ def tile_kanlayer_t_kernel(tc, x, base_weight, spline_weight, grad_out, out):
                 out=out[512 * bc : 512 * bc + 512, P * j : P * j + P].rearrange("(r p) i -> p r i", p=P), in_=ot[:]
             )
 
-        x_transpose(0, 0)
-        x_copy(0, 0)
+        x_transpose(0)
+        x_copy(0)
         g_transpose(0, 0)
         clamps(0)
+        func_s(0, 0)
         g_copy(0, 0, True)
         g_transpose(0, 1)
-        g_copy(0, 1, False)
+        load_g(2)
+        g_copy(0, 1, True)
+        func_s(0, 1)
         g_quantise(0)
-        w_regroup(0, 0, [("v", 1), ("s", 1), ("g", 2)])
-        w_regroup(0, 1, [("v", 2), ("g", 2)])
-        w_negate(0)
+        func_s(0, 2)
+        w_regroup(0, 0, [("v", 2), ("g", 1)])
+        func_s(0, 3)
+        w_regroup(0, 1, [("v", 1), ("g", 2)])
         w_quantise(0, 0)
-        func_s(0)
-        x_transpose(1, 0)
-        g_transpose(1, 0)
-        g_copy(1, 0, True)
-        g_transpose(1, 1)
-        x_copy(1, 0)
+        x_transpose(1)
+        x_copy(1)
+        w_regroup(0, 2, [("v", 1), ("g", 1), ("n", 1)])
+        func_v(0, 1, 2)
         w_quantise(0, 1)
-        w_quantise_negated(0)
-        g_copy(1, 1, False)
-        for q in range(LEAD):
-            issue_mx(q)
+        func_v(0, 2, 4)
         clamps(1)
-        func_v(0)
+        w_quantise(0, 2)
+        func_v(0, 4, 5)
+        for q in range(2):
+            issue_mx(q)
+        g_transpose(1, 0)
+        g_copy(1, 0, False)
+        g_transpose(1, 1)
+        g_copy(1, 1, False)
+        load_g(3)
+        load_w(2)
+        load_w(3)
+        for q in range(2, LEAD):
+            issue_mx(q)
         base_regroup()
-        g_quantise(1)
+        x_transpose(2)
+        x_copy(2)
+        base_quantise()
         for t in range(NTILES):
-            if t == 0:
-                base_quantise()
             if t < 2:
-                x_transpose(t + 2, 0)
                 g_transpose(t + 2, 0)
-                x_copy(t + 2, 0)
-                g_transpose(t + 2, 1)
-                g_copy(t + 2, 0, False)
-                g_copy(t + 2, 1, False)
-            elif t < 6:
-                x_transpose(t - 2, 1)
-                x_copy(t - 2, 1)
             if t + 1 < NTILES:
-                func_s(t + 1)
-            if t in (1, 2):
-                g_quantise(t + 1)
-            jn = t // 4 + 1
+                func_s(t + 1, 0)
+                func_s(t + 1, 1)
+            if t >= 1:
+                finish(t - 1)
+            if t < 2:
+                g_copy(t + 2, 0, False)
+            if t + 1 < NTILES:
+                func_s(t + 1, 2)
+                func_s(t + 1, 3)
+            jn, c = t // 4 + 1, t % 4
             if jn < 4:
-                if t % 4 == 1:
-                    w_regroup(jn, 0, [("g", 4)])
-                if t % 4 == 2:
-                    w_quantise(jn, 0)
-                    w_regroup(jn, 1, [("g", 4)])
-                    w_negate(jn)
-                if t % 4 == 3:
-                    w_quantise(jn, 1)
-                    w_quantise_negated(jn)
+                if c >= 1:
+                    w_quantise(jn, c - 1)
+                if c < 2:
+                    w_regroup(jn, c, [("g", 3)])
+                elif c == 2:
+                    w_regroup(jn, c, [("g", 2), ("n", 1)])
             for p in range(NPLANES):
                 q = NPLANES * t + p
                 consume(q)
-                if p == 1 and t >= 1:
-                    finish(t - 1)
+                if p == 0 and t < 3:
+                    g_quantise(t + 1)
+                if p == 2 and t < 2:
+                    g_transpose(t + 2, 1)
+                    g_copy(t + 2, 1, False)
+                if p == 3:
+                    plane_add(t)
+                if p == 4 and t + 3 < NTILES:
+                    x_transpose(t + 3)
+                    x_copy(t + 3)
                 if q + LEAD < NPLANES * NTILES:
                     issue_mx(q + LEAD)
+            adder(t)
             if t + 2 < NTILES:
                 clamps(t + 2)
-            plane_add(t)
-            adder(t)
             if t + 1 < NTILES:
-                func_v(t + 1)
+                func_v(t + 1, 1, 5)
         finish(NTILES - 1)

@@ -23,8 +23,13 @@ Q = 6.25
 NTILES = 16
 LEAD = 6
 ADD = [None, 1.5, 0.5, -0.5, -1.5, None]
-PLANES = [0, 1, 2, 3, 4, 5, "c"]
-NPLANES = len(PLANES)
+NPLANES = 7
+
+
+def plane(q):
+    t, n = q // NPLANES, q % NPLANES
+    order = [0, 1, 2, 3, 4, 5, "c"] if t == 0 else ["c", 0, 1, 2, 3, 4, 5]
+    return t, order[n]
 
 
 def tile_kanlayer_t_kernel(tc, x, base_weight, spline_weight, grad_out, out):
@@ -90,7 +95,7 @@ def tile_kanlayer_t_kernel(tc, x, base_weight, spline_weight, grad_out, out):
         wgs = {}
 
         def g_transpose(bc, c2):
-            xt = aux.tile([P, 2, 2, P], F32, tag="aux", name="xt")
+            xt = psum.tile([P, 2, 2, P], F32, tag="mx", name="xt")
             xts[(bc, c2)] = xt
             for n2 in range(2):
                 gw = g_sbs[bc][:, 2 * c2 + n2, :].bitcast(F32)
@@ -237,7 +242,7 @@ def tile_kanlayer_t_kernel(tc, x, base_weight, spline_weight, grad_out, out):
             )
 
         def issue_mx(q):
-            t, p = q // NPLANES, PLANES[q % NPLANES]
+            t, p = plane(q)
             j, bc = t // 4, t % 4
             bank = psum.tile([P, 512], F32, tag="mx", name="bank")
             banks[q] = bank
@@ -251,7 +256,7 @@ def tile_kanlayer_t_kernel(tc, x, base_weight, spline_weight, grad_out, out):
                 mx(bank, j, bc, 1, p + 2, False, True)
 
         def consume(q):
-            t, p = q // NPLANES, PLANES[q % NPLANES]
+            t, p = plane(q)
             fn = fns[t]
             bank = banks[q]
             if p == "c":
@@ -267,23 +272,29 @@ def tile_kanlayer_t_kernel(tc, x, base_weight, spline_weight, grad_out, out):
                     out=fn[:, p, :], in0=fn[:, p, :], scalar=ADD[p], in1=bank[:], op0=ALU.add, op1=ALU.mult
                 )
 
-        def plane_add(t):
-            fn = fns[t]
-            nc.vector.tensor_tensor(out=fn[:, 0, :], in0=fn[:, 0, :], in1=fn[:, 1, :], op=ALU.add)
+        def plane_adds(t):
+            fn, av = fns[t], avs[t + 1]
+            for n in range(2):
+                nc.gpsimd.tensor_tensor(out=av[:, n, :], in0=fn[:, 2 * n, :], in1=fn[:, 2 * n + 1, :], op=ALU.add)
 
         def adder(t):
             fn = fns[t]
+            if t + 1 < NTILES:
+                av = avs[t + 1]
+                planes = [fn[:, 4, :], fn[:, 5, :], fn[:, 6, :], av[:, 0, :], av[:, 1, :]]
+            else:
+                planes = [fn[:, a, :] for a in range(7)]
             ob = aux.tile([P, 4, P], F32, tag="aux", name="ob")
             obs[t] = ob
             for r in range(4):
-                for a in (0, 2, 3, 4, 5, 6):
+                for n, plane in enumerate(planes):
                     nc.tensor.matmul(
                         out=ob[:, r, :],
-                        lhsT=fn[:, a, P * r : P * r + P],
+                        lhsT=plane[:, P * r : P * r + P],
                         rhs=ident[:],
                         is_transpose=True,
-                        start=(a == 0),
-                        stop=(a == 6),
+                        start=(n == 0),
+                        stop=(n == len(planes) - 1),
                     )
 
         def finish(t):
@@ -328,20 +339,27 @@ def tile_kanlayer_t_kernel(tc, x, base_weight, spline_weight, grad_out, out):
         load_g(3)
         load_w(2)
         load_w(3)
+        x_transpose(2)
         for q in range(2, LEAD):
             issue_mx(q)
+        x_transpose(3)
         base_regroup()
-        x_transpose(2)
         x_copy(2)
         base_quantise()
+        g_quantise(1)
         for t in range(NTILES):
+            if t >= 1:
+                consume(NPLANES * t)
+                plane_adds(t - 1)
+            if t >= 2:
+                finish(t - 2)
+            if t + 3 < NTILES:
+                x_copy(t + 3)
             if t < 2:
                 g_transpose(t + 2, 0)
             if t + 1 < NTILES:
                 func_s(t + 1, 0)
                 func_s(t + 1, 1)
-            if t >= 1:
-                finish(t - 1)
             if t < 2:
                 g_copy(t + 2, 0, False)
             if t + 1 < NTILES:
@@ -349,30 +367,31 @@ def tile_kanlayer_t_kernel(tc, x, base_weight, spline_weight, grad_out, out):
                 func_s(t + 1, 3)
             jn, c = t // 4 + 1, t % 4
             if jn < 4:
-                if c >= 1:
-                    w_quantise(jn, c - 1)
                 if c < 2:
                     w_regroup(jn, c, [("g", 3)])
                 elif c == 2:
                     w_regroup(jn, c, [("g", 2), ("n", 1)])
-            for p in range(NPLANES):
-                q = NPLANES * t + p
-                consume(q)
-                if p == 0 and t < 3:
-                    g_quantise(t + 1)
-                if p == 2 and t < 2:
+            for n in range(NPLANES):
+                q = NPLANES * t + n
+                if n > 0 or t == 0:
+                    consume(q)
+                if n == 2 and t < 2:
                     g_transpose(t + 2, 1)
                     g_copy(t + 2, 1, False)
-                if p == 3:
-                    plane_add(t)
-                if p == 4 and t + 3 < NTILES:
-                    x_transpose(t + 3)
-                    x_copy(t + 3)
+                if n == 3 and t >= 1:
+                    adder(t - 1)
+                if n == 3 and t + 4 < NTILES:
+                    x_transpose(t + 4)
                 if q + LEAD < NPLANES * NTILES:
                     issue_mx(q + LEAD)
-            adder(t)
             if t + 2 < NTILES:
                 clamps(t + 2)
             if t + 1 < NTILES:
                 func_v(t + 1, 1, 5)
+            if t < 2:
+                g_quantise(t + 2)
+            if jn < 4 and c < 3:
+                w_quantise(jn, c)
+        finish(NTILES - 2)
+        adder(NTILES - 1)
         finish(NTILES - 1)

@@ -199,19 +199,19 @@ def tile_kanlayer_t_kernel(tc, x, base_weight, spline_weight, grad_out, out):
             cl, zt = cls[t], zts[t]
             act = nc.scalar.activation
             if part == 0:
-                avs[t] = avp.tile([P, 4, 512], F32, name="av")
-                fns[t] = fnp.tile([P, 7, 512], F32, name="fn")
-            av, fn = avs[t], fns[t]
-            if part == 0:
+                fn = fnp.tile([P, 7, 512], F32, name="fn")
+                fns[t] = fn
                 act(out=fn[:, 0, :], in_=xs, func=ACT.Relu, scale=-S, bias=S * XI[1])
                 act(out=fn[:, 5, :], in_=xs, func=ACT.Relu, scale=S, bias=-S * XI[4])
                 act(out=fn[:, 0, :], in_=fn[:, 0, :], func=ACT.Square, scale=1.0, bias=0.0)
                 act(out=fn[:, 5, :], in_=fn[:, 5, :], func=ACT.Square, scale=1.0, bias=0.0)
             elif part == 1:
+                av = avp.tile([P, 4, 512], F32, name="av")
+                avs[t] = av
                 act(out=av[:, 0, :], in_=zt[:, 0, :], func=ACT.Abs, scale=Q / H, bias=0.0)
                 act(out=av[:, 3, :], in_=zt[:, 3, :], func=ACT.Abs, scale=Q / H, bias=0.0)
             else:
-                k = part
+                k, av = part, avs[t]
                 act(out=av[:, k - 1, :], in_=cl[:, k - 2, :], func=ACT.Abs, scale=Q / H, bias=-Q * XI[k] / H)
                 act(out=zt[:, k - 1, :], in_=cl[:, k - 2, :], func=ACT.Identity, scale=1.0, bias=-XI[k])
 
@@ -277,16 +277,17 @@ def tile_kanlayer_t_kernel(tc, x, base_weight, spline_weight, grad_out, out):
             for n in range(2):
                 nc.gpsimd.tensor_tensor(out=av[:, n, :], in0=fn[:, 2 * n, :], in1=fn[:, 2 * n + 1, :], op=ALU.add)
 
-        def adder(t):
+        def adder(t, rows):
             fn = fns[t]
             if t + 1 < NTILES:
                 av = avs[t + 1]
                 planes = [fn[:, 4, :], fn[:, 5, :], fn[:, 6, :], av[:, 0, :], av[:, 1, :]]
             else:
                 planes = [fn[:, a, :] for a in range(7)]
-            ob = aux.tile([P, 4, P], F32, tag="aux", name="ob")
-            obs[t] = ob
-            for r in range(4):
+            if 0 in rows:
+                obs[t] = aux.tile([P, 4, P], F32, tag="aux", name="ob")
+            ob = obs[t]
+            for r in rows:
                 for n, plane in enumerate(planes):
                     nc.tensor.matmul(
                         out=ob[:, r, :],
@@ -351,20 +352,21 @@ def tile_kanlayer_t_kernel(tc, x, base_weight, spline_weight, grad_out, out):
             if t >= 1:
                 consume(NPLANES * t)
                 plane_adds(t - 1)
-            if t >= 2:
-                finish(t - 2)
             if t + 3 < NTILES:
                 x_copy(t + 3)
             if t < 2:
                 g_transpose(t + 2, 0)
             if t + 1 < NTILES:
-                func_s(t + 1, 0)
                 func_s(t + 1, 1)
             if t < 2:
                 g_copy(t + 2, 0, False)
             if t + 1 < NTILES:
                 func_s(t + 1, 2)
+            if t >= 2:
+                finish(t - 2)
+            if t + 1 < NTILES:
                 func_s(t + 1, 3)
+                func_s(t + 1, 0)
             jn, c = t // 4 + 1, t % 4
             if jn < 4:
                 if c < 2:
@@ -379,9 +381,11 @@ def tile_kanlayer_t_kernel(tc, x, base_weight, spline_weight, grad_out, out):
                     g_transpose(t + 2, 1)
                     g_copy(t + 2, 1, False)
                 if n == 3 and t >= 1:
-                    adder(t - 1)
+                    adder(t - 1, (0, 1))
                 if n == 3 and t + 4 < NTILES:
                     x_transpose(t + 4)
+                if n == 6 and t >= 1:
+                    adder(t - 1, (2, 3))
                 if q + LEAD < NPLANES * NTILES:
                     issue_mx(q + LEAD)
             if t + 2 < NTILES:
@@ -393,5 +397,5 @@ def tile_kanlayer_t_kernel(tc, x, base_weight, spline_weight, grad_out, out):
             if jn < 4 and c < 3:
                 w_quantise(jn, c)
         finish(NTILES - 2)
-        adder(NTILES - 1)
+        adder(NTILES - 1, (0, 1, 2, 3))
         finish(NTILES - 1)

@@ -28,7 +28,7 @@ NPLANES = 7
 
 def plane(q):
     t, n = q // NPLANES, q % NPLANES
-    order = [0, 1, 2, 3, 4, 5, "c"] if t == 0 else ["c", 0, 1, 2, 3, 4, 5]
+    order = [0, 1, 2, 3, 4, 5, "c"] if t == 0 else [0, 1, "c", 2, 3, 4, 5]
     return t, order[n]
 
 
@@ -38,8 +38,8 @@ def tile_kanlayer_t_kernel(tc, x, base_weight, spline_weight, grad_out, out):
         keep = ctx.enter_context(tc.tile_pool(name="keep", bufs=1))
         grp = ctx.enter_context(tc.tile_pool(name="grp", bufs=2))
         clp = ctx.enter_context(tc.tile_pool(name="clp", bufs=2))
-        avp = ctx.enter_context(tc.tile_pool(name="avp", bufs=2))
-        fnp = ctx.enter_context(tc.tile_pool(name="fnp", bufs=3))
+        avp = ctx.enter_context(tc.tile_pool(name="avp", bufs=3))
+        fnp = ctx.enter_context(tc.tile_pool(name="fnp", bufs=4))
         outp = ctx.enter_context(tc.tile_pool(name="outp", bufs=3))
         psum = ctx.enter_context(tc.psum_pool(name="psum", bufs=LEAD))
         aux = ctx.enter_context(tc.psum_pool(name="aux", bufs=2))
@@ -49,15 +49,14 @@ def tile_kanlayer_t_kernel(tc, x, base_weight, spline_weight, grad_out, out):
         make_identity(nc, ident[:])
         ident_bf = keep.tile([P, P], BF16)
         make_identity(nc, ident_bf[:])
-        w_codes = keep.tile([P, 4, L + 1, P], U32, align_bytes=64)
-        w_scales = keep.tile([P, 4, L + 1, P], U8, align_bytes=64)
-        wb_codes = keep.tile([P, I], U32, align_bytes=64)
+        w_codes = keep.tile([P, 4, L + 1, P], U32, align_bytes=256)
+        w_scales = keep.tile([P, 4, L + 1, P], U8, align_bytes=256)
+        wb_codes = keep.tile([P, I], U32, align_bytes=256)
         wb_scales = keep.tile([P, I], U8, align_bytes=64)
-        g_codes = keep.tile([P, 2, B], U32, align_bytes=64)
-        g_scales = keep.tile([P, 2, B], U8, align_bytes=64)
+        g_codes = keep.tile([P, 2, B], U32, align_bytes=256)
+        g_scales = keep.tile([P, 2, B], U8, align_bytes=256)
         xT = keep.tile([P, 4, B], BF16)
         x_sb = keep.tile([P, 16, I], BF16)
-        w_raw = keep.tile([P, 4, 4, L * P], BF16)
         wb_raw = keep.tile([P, 4, I], BF16)
 
         g_view = grad_out.rearrange("(n p) o -> p n o", p=P)
@@ -74,9 +73,13 @@ def tile_kanlayer_t_kernel(tc, x, base_weight, spline_weight, grad_out, out):
         def load_x(bc):
             nc.sync.dma_start(out=x_sb[:, 4 * bc : 4 * bc + 4, :], in_=x_view[:, 4 * bc : 4 * bc + 4, :])
 
+        w_raws = {}
+
         def load_w(j):
+            w_raw = grp.tile([P, 4, L * P], BF16, tag="w_raw", name="w_raw")
+            w_raws[j] = w_raw
             nc.sync.dma_start(
-                out=w_raw[:, j], in_=sw[:, L * P * j : L * P * (j + 1)].rearrange("(q t) c -> q t c", t=4)
+                out=w_raw[:], in_=sw[:, L * P * j : L * P * (j + 1)].rearrange("(q t) c -> q t c", t=4)
             )
 
         load_x(0)
@@ -136,7 +139,7 @@ def tile_kanlayer_t_kernel(tc, x, base_weight, spline_weight, grad_out, out):
         def w_regroup(j, c, engines):
             wg = grp.tile([P, 3, P, 4], BF16, align_bytes=64, tag="wg", name="wg")
             wgs[(j, c)] = wg
-            src = w_raw[:, j].rearrange("p t (i l) -> p i l t", l=L)
+            src = w_raws[j][:].rearrange("p t (i l) -> p i l t", l=L)
             dst = wg[:].rearrange("p l i t -> p i l t")
             k = 0
             for name, n in engines:
@@ -146,7 +149,7 @@ def tile_kanlayer_t_kernel(tc, x, base_weight, spline_weight, grad_out, out):
                 if name == "v":
                     nc.vector.tensor_copy(out=d, in_=s)
                 elif name == "s":
-                    nc.scalar.copy(out=d, in_=s)
+                    nc.scalar.activation(out=d, in_=s, func=ACT.Copy, scale=1.0 if l0 < L else -1.0)
                 elif name == "g":
                     nc.gpsimd.tensor_scalar(out=d, in0=s, scalar1=1.0, scalar2=0.0, op0=ALU.mult, op1=ALU.add)
                 else:
@@ -199,7 +202,7 @@ def tile_kanlayer_t_kernel(tc, x, base_weight, spline_weight, grad_out, out):
             cl, zt = cls[t], zts[t]
             act = nc.scalar.activation
             if part == 0:
-                fn = fnp.tile([P, 7, 512], F32, name="fn")
+                fn = fnp.tile([P, 6, 512], F32, name="fn")
                 fns[t] = fn
                 act(out=fn[:, 0, :], in_=xs, func=ACT.Relu, scale=-S, bias=S * XI[1])
                 act(out=fn[:, 5, :], in_=xs, func=ACT.Relu, scale=S, bias=-S * XI[4])
@@ -260,7 +263,7 @@ def tile_kanlayer_t_kernel(tc, x, base_weight, spline_weight, grad_out, out):
             fn = fns[t]
             bank = banks[q]
             if p == "c":
-                nc.scalar.copy(out=fn[:, 6, :], in_=bank[:])
+                nc.vector.tensor_tensor(out=fn[:, 0, :], in0=fn[:, 0, :], in1=bank[:], op=ALU.add)
             elif p == 0:
                 nc.vector.tensor_tensor(out=fn[:, 0, :], in0=fn[:, 0, :], in1=bank[:], op=ALU.mult)
             elif p == 5:
@@ -281,9 +284,9 @@ def tile_kanlayer_t_kernel(tc, x, base_weight, spline_weight, grad_out, out):
             fn = fns[t]
             if t + 1 < NTILES:
                 av = avs[t + 1]
-                planes = [fn[:, 4, :], fn[:, 5, :], fn[:, 6, :], av[:, 0, :], av[:, 1, :]]
+                planes = [fn[:, 4, :], fn[:, 5, :], av[:, 0, :], av[:, 1, :]]
             else:
-                planes = [fn[:, a, :] for a in range(7)]
+                planes = [fn[:, a, :] for a in range(6)]
             if 0 in rows:
                 obs[t] = aux.tile([P, 4, P], F32, tag="aux", name="ob")
             ob = obs[t]
@@ -318,74 +321,66 @@ def tile_kanlayer_t_kernel(tc, x, base_weight, spline_weight, grad_out, out):
         func_s(0, 1)
         g_quantise(0)
         func_s(0, 2)
-        w_regroup(0, 0, [("v", 2), ("g", 1)])
         func_s(0, 3)
-        w_regroup(0, 1, [("v", 1), ("g", 2)])
+        w_regroup(0, 0, [("v", 3)])
         w_quantise(0, 0)
+        w_regroup(0, 1, [("v", 3)])
+        w_quantise(0, 1)
         x_transpose(1)
         x_copy(1)
-        w_regroup(0, 2, [("v", 1), ("g", 1), ("n", 1)])
-        func_v(0, 1, 2)
-        w_quantise(0, 1)
-        func_v(0, 2, 4)
-        clamps(1)
-        w_quantise(0, 2)
-        func_v(0, 4, 5)
-        for q in range(2):
-            issue_mx(q)
         g_transpose(1, 0)
         g_copy(1, 0, False)
         g_transpose(1, 1)
         g_copy(1, 1, False)
         load_g(3)
+        w_regroup(0, 2, [("s", 2), ("s", 1)])
         load_w(2)
-        load_w(3)
-        x_transpose(2)
-        for q in range(2, LEAD):
+        for q in range(4):
             issue_mx(q)
-        x_transpose(3)
+        func_v(0, 1, 5)
+        w_quantise(0, 2)
         base_regroup()
+        for q in range(4, LEAD):
+            issue_mx(q)
+        x_transpose(2)
+        x_transpose(3)
         x_copy(2)
         base_quantise()
-        g_quantise(1)
+        clamps(1)
         for t in range(NTILES):
             if t >= 1:
-                consume(NPLANES * t)
                 plane_adds(t - 1)
-            if t + 3 < NTILES:
-                x_copy(t + 3)
-            if t < 2:
-                g_transpose(t + 2, 0)
             if t + 1 < NTILES:
                 func_s(t + 1, 1)
-            if t < 2:
-                g_copy(t + 2, 0, False)
-            if t + 1 < NTILES:
                 func_s(t + 1, 2)
             if t >= 2:
                 finish(t - 2)
             if t + 1 < NTILES:
                 func_s(t + 1, 3)
                 func_s(t + 1, 0)
+            if t + 3 < NTILES:
+                x_copy(t + 3)
             jn, c = t // 4 + 1, t % 4
             if jn < 4:
                 if c < 2:
                     w_regroup(jn, c, [("g", 3)])
                 elif c == 2:
                     w_regroup(jn, c, [("g", 2), ("n", 1)])
+                    if jn == 1:
+                        load_w(3)
             for n in range(NPLANES):
                 q = NPLANES * t + n
-                if n > 0 or t == 0:
-                    consume(q)
-                if n == 2 and t < 2:
-                    g_transpose(t + 2, 1)
-                    g_copy(t + 2, 1, False)
-                if n == 3 and t >= 1:
-                    adder(t - 1, (0, 1))
-                if n == 3 and t + 4 < NTILES:
-                    x_transpose(t + 4)
-                if n == 6 and t >= 1:
-                    adder(t - 1, (2, 3))
+                consume(q)
+                if q == 0:
+                    g_quantise(1)
+                if n in (1, 3) and t < 2:
+                    g_transpose(t + 2, n // 2)
+                    g_copy(t + 2, n // 2, False)
+                if n == 2:
+                    if t >= 1:
+                        adder(t - 1, (0, 1, 2, 3))
+                    if t + 4 < NTILES:
+                        x_transpose(t + 4)
                 if q + LEAD < NPLANES * NTILES:
                     issue_mx(q + LEAD)
             if t + 2 < NTILES:

@@ -136,25 +136,18 @@ def tile_kanlayer_t_kernel(tc, x, base_weight, spline_weight, grad_out, out):
             j, bc = t // 4, t % 4
             nc.scalar.copy(out=xT[:, j, 512 * bc : 512 * bc + 512], in_=xps[t][:])
 
-        def w_regroup(j, c, engines):
-            wg = grp.tile([P, 3, P, 4], BF16, align_bytes=64, tag="wg", name="wg")
-            wgs[(j, c)] = wg
-            src = w_raws[j][:].rearrange("p t (i l) -> p i l t", l=L)
-            dst = wg[:].rearrange("p l i t -> p i l t")
-            k = 0
-            for name, n in engines:
-                l0 = 3 * c + k
-                d = dst[:, :, k : k + n, :]
-                s = src[:, :, l0 : l0 + n, :] if l0 < L else src[:, :, 6:7, :]
-                if name == "v":
-                    nc.vector.tensor_copy(out=d, in_=s)
-                elif name == "s":
-                    nc.scalar.activation(out=d, in_=s, func=ACT.Copy, scale=1.0 if l0 < L else -1.0)
-                elif name == "g":
-                    nc.gpsimd.tensor_scalar(out=d, in0=s, scalar1=1.0, scalar2=0.0, op0=ALU.mult, op1=ALU.add)
-                else:
-                    nc.gpsimd.tensor_scalar(out=d, in0=s, scalar1=-1.0, scalar2=0.0, op0=ALU.mult, op1=ALU.add)
-                k += n
+        def w_regroup(j, l, engine):
+            if l % 3 == 0:
+                wgs[(j, l // 3)] = grp.tile([P, 3, P, 4], BF16, align_bytes=64, tag="wg", name="wg")
+            src = w_raws[j][:].rearrange("p t (i l) -> p i l t", l=L)[:, :, l if l < L else 6, :]
+            dst = wgs[(j, l // 3)][:, l % 3]
+            sign = 1.0 if l < L else -1.0
+            if engine == "v":
+                nc.vector.tensor_copy(out=dst, in_=src)
+            elif engine == "s":
+                nc.scalar.activation(out=dst, in_=src, func=ACT.Copy, scale=sign)
+            else:
+                nc.gpsimd.tensor_scalar(out=dst, in0=src, scalar1=sign, scalar2=0.0, op0=ALU.mult, op1=ALU.add)
 
         def w_quantise(j, c):
             for k, n in ((0, 2), (2, 1)):
@@ -322,9 +315,11 @@ def tile_kanlayer_t_kernel(tc, x, base_weight, spline_weight, grad_out, out):
         g_quantise(0)
         func_s(0, 2)
         func_s(0, 3)
-        w_regroup(0, 0, [("v", 3)])
+        for l in range(3):
+            w_regroup(0, l, "v")
         w_quantise(0, 0)
-        w_regroup(0, 1, [("v", 3)])
+        for l in range(3, 6):
+            w_regroup(0, l, "v")
         w_quantise(0, 1)
         x_transpose(1)
         x_copy(1)
@@ -333,7 +328,8 @@ def tile_kanlayer_t_kernel(tc, x, base_weight, spline_weight, grad_out, out):
         g_transpose(1, 1)
         g_copy(1, 1, False)
         load_g(3)
-        w_regroup(0, 2, [("s", 2), ("s", 1)])
+        for l in range(6, 9):
+            w_regroup(0, l, "s")
         load_w(2)
         for q in range(4):
             issue_mx(q)
@@ -345,7 +341,6 @@ def tile_kanlayer_t_kernel(tc, x, base_weight, spline_weight, grad_out, out):
         x_transpose(2)
         x_transpose(3)
         x_copy(2)
-        base_quantise()
         clamps(1)
         for t in range(NTILES):
             if t >= 1:
@@ -361,18 +356,14 @@ def tile_kanlayer_t_kernel(tc, x, base_weight, spline_weight, grad_out, out):
             if t + 3 < NTILES:
                 x_copy(t + 3)
             jn, c = t // 4 + 1, t % 4
-            if jn < 4:
-                if c < 2:
-                    w_regroup(jn, c, [("g", 3)])
-                elif c == 2:
-                    w_regroup(jn, c, [("g", 2), ("n", 1)])
-                    if jn == 1:
-                        load_w(3)
+            weights = jn < 4 and c < 3
+            if weights:
+                w_regroup(jn, 3 * c, "s")
+                w_regroup(jn, 3 * c + 1, "s")
+                w_regroup(jn, 3 * c + 2, "s")
             for n in range(NPLANES):
                 q = NPLANES * t + n
                 consume(q)
-                if q == 0:
-                    g_quantise(1)
                 if n in (1, 3) and t < 2:
                     g_transpose(t + 2, n // 2)
                     g_copy(t + 2, n // 2, False)
@@ -381,7 +372,11 @@ def tile_kanlayer_t_kernel(tc, x, base_weight, spline_weight, grad_out, out):
                         adder(t - 1, (0, 1, 2, 3))
                     if t + 4 < NTILES:
                         x_transpose(t + 4)
-                if q + LEAD < NPLANES * NTILES:
+                if q == 1:
+                    base_quantise()
+                    issue_mx(LEAD)
+                    g_quantise(1)
+                if 0 < q < NPLANES * NTILES - LEAD:
                     issue_mx(q + LEAD)
             if t + 2 < NTILES:
                 clamps(t + 2)
@@ -389,8 +384,10 @@ def tile_kanlayer_t_kernel(tc, x, base_weight, spline_weight, grad_out, out):
                 func_v(t + 1, 1, 5)
             if t < 2:
                 g_quantise(t + 2)
-            if jn < 4 and c < 3:
+            if weights:
                 w_quantise(jn, c)
+            if t == 2:
+                load_w(3)
         finish(NTILES - 2)
         adder(NTILES - 1, (0, 1, 2, 3))
         finish(NTILES - 1)

@@ -136,26 +136,23 @@ def tile_kanlayer_t_kernel(tc, x, base_weight, spline_weight, grad_out, out):
             j, bc = t // 4, t % 4
             nc.scalar.copy(out=xT[:, j, 512 * bc : 512 * bc + 512], in_=xps[t][:])
 
-        def w_regroup(j, l, engine):
-            if l % 3 == 0:
-                wgs[(j, l // 3)] = grp.tile([P, 3, P, 4], BF16, align_bytes=64, tag="wg", name="wg")
-            src = w_raws[j][:].rearrange("p t (i l) -> p i l t", l=L)[:, :, l if l < L else 6, :]
-            dst = wgs[(j, l // 3)][:, l % 3]
-            sign = 1.0 if l < L else -1.0
-            if engine == "v":
-                nc.vector.tensor_copy(out=dst, in_=src)
-            elif engine == "s":
-                nc.scalar.activation(out=dst, in_=src, func=ACT.Copy, scale=sign)
-            else:
-                nc.gpsimd.tensor_scalar(out=dst, in0=src, scalar1=sign, scalar2=0.0, op0=ALU.mult, op1=ALU.add)
+        def w_regroup(j, c, copy):
+            wg = grp.tile([P, 3, P, 4], BF16, align_bytes=64, tag="wg", name="wg")
+            wgs[(j, c)] = wg
+            n = min(3, L - 3 * c)
+            src = w_raws[j][:].rearrange("p t (i l) -> p i l t", l=L)
+            copy(out=wg[:].rearrange("p l i t -> p i l t")[:, :, 0:n, :], in_=src[:, :, 3 * c : 3 * c + n, :])
 
         def w_quantise(j, c):
+            wg = wgs[(j, c)]
+            if c == 2:
+                nc.vector.tensor_scalar(out=wg[:, 2], in0=wg[:, 0], scalar1=-1.0, scalar2=None, op0=ALU.mult)
             for k, n in ((0, 2), (2, 1)):
                 cols = slice(3 * c + k, 3 * c + k + n)
                 nc.vector.quantize_mx(
                     out=w_codes[:, j, cols].rearrange("p l i -> p (l i)").bitcast(E4X4),
                     scales=w_scales[:, j, cols].rearrange("p l i -> p (l i)"),
-                    in_=wgs[(j, c)][:, k : k + n].rearrange("p l i t -> p (l i t)"),
+                    in_=wg[:, k : k + n].rearrange("p l i t -> p (l i t)"),
                 )
 
         def base_regroup():
@@ -315,11 +312,9 @@ def tile_kanlayer_t_kernel(tc, x, base_weight, spline_weight, grad_out, out):
         g_quantise(0)
         func_s(0, 2)
         func_s(0, 3)
-        for l in range(3):
-            w_regroup(0, l, "v")
+        w_regroup(0, 0, nc.vector.tensor_copy)
         w_quantise(0, 0)
-        for l in range(3, 6):
-            w_regroup(0, l, "v")
+        w_regroup(0, 1, nc.vector.tensor_copy)
         w_quantise(0, 1)
         x_transpose(1)
         x_copy(1)
@@ -328,8 +323,7 @@ def tile_kanlayer_t_kernel(tc, x, base_weight, spline_weight, grad_out, out):
         g_transpose(1, 1)
         g_copy(1, 1, False)
         load_g(3)
-        for l in range(6, 9):
-            w_regroup(0, l, "s")
+        w_regroup(0, 2, nc.scalar.copy)
         load_w(2)
         for q in range(4):
             issue_mx(q)
@@ -358,9 +352,7 @@ def tile_kanlayer_t_kernel(tc, x, base_weight, spline_weight, grad_out, out):
             jn, c = t // 4 + 1, t % 4
             weights = jn < 4 and c < 3
             if weights:
-                w_regroup(jn, 3 * c, "s")
-                w_regroup(jn, 3 * c + 1, "s")
-                w_regroup(jn, 3 * c + 2, "s")
+                w_regroup(jn, c, nc.scalar.copy)
             for n in range(NPLANES):
                 q = NPLANES * t + n
                 consume(q)

from contextlib import ExitStack

import concourse.mybir as mybir
from concourse.masks import make_identity

F32 = mybir.dt.float32
BF16 = mybir.dt.bfloat16
U32 = mybir.dt.uint32
U8 = mybir.dt.uint8
E4X4 = mybir.dt.float8_e4m3fn_x4
E5X4 = mybir.dt.float8_e5m2_x4
ALU = mybir.AluOpType
ACT = mybir.ActivationFunctionType

P = 128
B, I, O, L = 2048, 512, 512, 8
FLOPS = 2 * B * O * (I + I * L)

H = 0.4
XI = [-1.0 + H * k for k in range(6)]
S = 2.5 ** 0.5 / H
Q = 6.25
NTILES = 16
LEAD = 6
ADD = [None, 1.5, 0.5, -0.5, -1.5, None]
NPLANES = 7


def plane(q):
    t, n = q // NPLANES, q % NPLANES
    order = [0, 1, 2, 3, 4, 5, "c"] if t == 0 else [0, 1, "c", 2, 3, 4, 5]
    return t, order[n]


def tile_kanlayer_t_kernel(tc, x, base_weight, spline_weight, grad_out, out):
    nc = tc.nc
    with ExitStack() as ctx:
        keep = ctx.enter_context(tc.tile_pool(name="keep", bufs=1))
        grp = ctx.enter_context(tc.tile_pool(name="grp", bufs=2))
        clp = ctx.enter_context(tc.tile_pool(name="clp", bufs=2))
        avp = ctx.enter_context(tc.tile_pool(name="avp", bufs=3))
        fnp = ctx.enter_context(tc.tile_pool(name="fnp", bufs=4))
        outp = ctx.enter_context(tc.tile_pool(name="outp", bufs=3))
        psum = ctx.enter_context(tc.psum_pool(name="psum", bufs=LEAD))
        aux = ctx.enter_context(tc.psum_pool(name="aux", bufs=2))
        ctx.enter_context(tc.manual_schedule())

        ident = keep.tile([P, P], F32)
        make_identity(nc, ident[:])
        ident_bf = keep.tile([P, P], BF16)
        make_identity(nc, ident_bf[:])
        w_codes = keep.tile([P, 4, L + 1, P], U32, align_bytes=256)
        w_scales = keep.tile([P, 4, L + 1, P], U8, align_bytes=256)
        wb_codes = keep.tile([P, I], U32, align_bytes=256)
        wb_scales = keep.tile([P, I], U8, align_bytes=64)
        g_codes = keep.tile([P, 2, B], U32, align_bytes=256)
        g_scales = keep.tile([P, 2, B], U8, align_bytes=256)
        xT = keep.tile([P, 4, B], BF16)
        x_sb = keep.tile([P, 16, I], BF16)
        wb_raw = keep.tile([P, 4, I], BF16)

        g_view = grad_out.rearrange("(n p) o -> p n o", p=P)
        x_view = x.rearrange("(n p) i -> p n i", p=P)
        sw = spline_weight.rearrange("o i l -> o (i l)")

        g_sbs = {}

        def load_g(bc):
            g_sb = grp.tile([P, 4, O], BF16, tag="g_sb", name="g_sb")
            g_sbs[bc] = g_sb
            nc.sync.dma_start(out=g_sb[:], in_=g_view[:, 4 * bc : 4 * bc + 4, :])

        def load_x(bc):
            nc.sync.dma_start(out=x_sb[:, 4 * bc : 4 * bc + 4, :], in_=x_view[:, 4 * bc : 4 * bc + 4, :])

        w_raws = {}

        def load_w(j):
            w_raw = grp.tile([P, 4, L * P], BF16, tag="w_raw", name="w_raw")
            w_raws[j] = w_raw
            nc.sync.dma_start(
                out=w_raw[:], in_=sw[:, L * P * j : L * P * (j + 1)].rearrange("(q t) c -> q t c", t=4)
            )

        load_x(0)
        load_g(0)
        load_w(0)
        load_x(1)
        load_g(1)
        nc.sync.dma_start(out=wb_raw[:], in_=base_weight.rearrange("(q t) c -> q t c", t=4))
        load_x(2)
        load_w(1)
        load_x(3)

        ggs = {}
        xts = {}
        xps = {}
        wgs = {}

        def g_transpose(bc, c2):
            xt = psum.tile([P, 2, 2, P], F32, tag="mx", name="xt")
            xts[(bc, c2)] = xt
            for n2 in range(2):
                gw = g_sbs[bc][:, 2 * c2 + n2, :].bitcast(F32)
                for u in range(2):
                    nc.tensor.transpose(xt[:, n2, u, :], gw[:, u : 2 * P : 2], ident[:])

        def g_copy(bc, c2, on_vector):
            if c2 == 0:
                ggs[bc] = grp.tile([P, 512, 4], BF16, align_bytes=64, tag="gg", name="gg")
            ggf = ggs[bc][:].rearrange("p b t -> p (b t)").bitcast(F32).rearrange("p (b u) -> p b u", u=2)
            dst = ggf[:, 256 * c2 : 256 * c2 + 256, :].rearrange("p (n b) u -> p n b u", n=2)
            src = xts[(bc, c2)][:].rearrange("p n u b -> p n b u")
            if on_vector:
                nc.vector.tensor_copy(out=dst, in_=src)
            else:
                nc.scalar.copy(out=dst, in_=src)

        def g_quantise(bc):
            gg2 = grp.tile([P, 512, 4], BF16, align_bytes=64, tag="gg2", name="gg2")
            flat = ggs[bc][:].rearrange("p b t -> p (b t)")
            flat2 = gg2[:].rearrange("p b t -> p (b t)")
            nc.vector.tensor_scalar(out=flat2, in0=flat, scalar1=-0.5, scalar2=None, op0=ALU.mult)
            cols = slice(512 * bc, 512 * bc + 512)
            nc.vector.quantize_mx(out=g_codes[:, 0, cols].bitcast(E5X4), scales=g_scales[:, 0, cols], in_=flat)
            nc.vector.quantize_mx(out=g_codes[:, 1, cols].bitcast(E5X4), scales=g_scales[:, 1, cols], in_=flat2)

        def x_transpose(t):
            j, bc = t // 4, t % 4
            xp = aux.tile([P, 512], BF16, tag="aux", name="xp")
            xps[t] = xp
            for r in range(4):
                nc.tensor.transpose(xp[:, P * r : P * r + P], x_sb[:, 4 * bc + r, P * j : P * j + P], ident_bf[:])

        def x_copy(t):
            j, bc = t // 4, t % 4
            nc.scalar.copy(out=xT[:, j, 512 * bc : 512 * bc + 512], in_=xps[t][:])

        def w_regroup(j, c, copy):
            wg = grp.tile([P, 3, P, 4], BF16, align_bytes=64, tag="wg", name="wg")
            wgs[(j, c)] = wg
            n = min(3, L - 3 * c)
            src = w_raws[j][:].rearrange("p t (i l) -> p i l t", l=L)
            copy(out=wg[:].rearrange("p l i t -> p i l t")[:, :, 0:n, :], in_=src[:, :, 3 * c : 3 * c + n, :])

        def w_quantise(j, c):
            wg = wgs[(j, c)]
            if c == 2:
                nc.vector.tensor_scalar(out=wg[:, 2], in0=wg[:, 0], scalar1=-1.0, scalar2=None, op0=ALU.mult)
            for k, n in ((0, 2), (2, 1)):
                cols = slice(3 * c + k, 3 * c + k + n)
                nc.vector.quantize_mx(
                    out=w_codes[:, j, cols].rearrange("p l i -> p (l i)").bitcast(E4X4),
                    scales=w_scales[:, j, cols].rearrange("p l i -> p (l i)"),
                    in_=wg[:, k : k + n].rearrange("p l i t -> p (l i t)"),
                )

        def base_regroup():
            wbg = keep.tile([P, 512, 4], BF16, align_bytes=64, name="wbg")
            wgs["b"] = wbg
            nc.scalar.copy(out=wbg[:], in_=wb_raw[:].rearrange("p t i -> p i t"))

        def base_quantise():
            nc.vector.quantize_mx(
                out=wb_codes[:].bitcast(E4X4), scales=wb_scales[:], in_=wgs["b"][:].rearrange("p i t -> p (i t)")
            )

        cls = {}
        zts = {}
        avs = {}
        fns = {}
        banks = {}
        obs = {}

        def xs_of(t):
            j, bc = t // 4, t % 4
            return xT[:, j, 512 * bc : 512 * bc + 512]

        def clamps(t):
            xs = xs_of(t)
            zt = clp.tile([P, 4, 512], F32, name="zt")
            cl = clp.tile([P, 2, 512], F32, name="cl")
            zts[t], cls[t] = zt, cl
            ts = nc.vector.tensor_scalar
            ts(out=zt[:, 0, :], in0=xs, scalar1=XI[1], scalar2=H, op0=ALU.subtract, op1=ALU.min)
            ts(out=zt[:, 3, :], in0=xs, scalar1=XI[4], scalar2=-H, op0=ALU.subtract, op1=ALU.max)
            for k in (2, 3):
                ts(out=cl[:, k - 2, :], in0=xs, scalar1=XI[k - 1], scalar2=XI[k + 1], op0=ALU.max, op1=ALU.min)

        def func_s(t, part):
            xs = xs_of(t)
            cl, zt = cls[t], zts[t]
            act = nc.scalar.activation
            if part == 0:
                fn = fnp.tile([P, 6, 512], F32, name="fn")
                fns[t] = fn
                act(out=fn[:, 0, :], in_=xs, func=ACT.Relu, scale=-S, bias=S * XI[1])
                act(out=fn[:, 5, :], in_=xs, func=ACT.Relu, scale=S, bias=-S * XI[4])
                act(out=fn[:, 0, :], in_=fn[:, 0, :], func=ACT.Square, scale=1.0, bias=0.0)
                act(out=fn[:, 5, :], in_=fn[:, 5, :], func=ACT.Square, scale=1.0, bias=0.0)
            elif part == 1:
                av = avp.tile([P, 4, 512], F32, name="av")
                avs[t] = av
                act(out=av[:, 0, :], in_=zt[:, 0, :], func=ACT.Abs, scale=Q / H, bias=0.0)
                act(out=av[:, 3, :], in_=zt[:, 3, :], func=ACT.Abs, scale=Q / H, bias=0.0)
            else:
                k, av = part, avs[t]
                act(out=av[:, k - 1, :], in_=cl[:, k - 2, :], func=ACT.Abs, scale=Q / H, bias=-Q * XI[k] / H)
                act(out=zt[:, k - 1, :], in_=cl[:, k - 2, :], func=ACT.Identity, scale=1.0, bias=-XI[k])

        def func_v(t, a, b):
            nc.vector.scalar_tensor_tensor(
                out=fns[t][:, a:b, :],
                in0=avs[t][:, a - 1 : b - 1, :],
                scalar=-2.0 * Q,
                in1=zts[t][:, a - 1 : b - 1, :],
                op0=ALU.add,
                op1=ALU.mult,
            )

        def mx(bank, j, bc, v, l, start, stop):
            gc = slice(512 * bc, 512 * bc + 512)
            if l <= L:
                lhsT, lhsT_scale = w_codes[:, j, l, :], w_scales[:, j, l, :]
            else:
                lhsT, lhsT_scale = wb_codes[:, P * j : P * j + P], wb_scales[:, P * j : P * j + P]
            nc.tensor.matmul_mx(
                out=bank[:],
                lhsT=lhsT.bitcast(E4X4),
                lhsT_scale=lhsT_scale,
                rhs=g_codes[:, v, gc].bitcast(E5X4),
                rhs_scale=g_scales[:, v, gc],
                start=start,
                stop=stop,
            )

        def issue_mx(q):
            t, p = plane(q)
            j, bc = t // 4, t % 4
            bank = psum.tile([P, 512], F32, tag="mx", name="bank")
            banks[q] = bank
            if p == "c":
                mx(bank, j, bc, 0, L + 1, True, False)
                mx(bank, j, bc, 1, L, False, False)
                mx(bank, j, bc, 1, 1, False, True)
            else:
                mx(bank, j, bc, 0, p + 1, True, False)
                mx(bank, j, bc, 1, p, False, False)
                mx(bank, j, bc, 1, p + 2, False, True)

        def consume(q):
            t, p = plane(q)
            fn = fns[t]
            bank = banks[q]
            if p == "c":
                nc.vector.tensor_tensor(out=fn[:, 0, :], in0=fn[:, 0, :], in1=bank[:], op=ALU.add)
            elif p == 0:
                nc.vector.tensor_tensor(out=fn[:, 0, :], in0=fn[:, 0, :], in1=bank[:], op=ALU.mult)
            elif p == 5:
                nc.vector.scalar_tensor_tensor(
                    out=fn[:, 5, :], in0=fn[:, 5, :], scalar=-1.0, in1=bank[:], op0=ALU.mult, op1=ALU.mult
                )
            else:
                nc.vector.scalar_tensor_tensor(
                    out=fn[:, p, :], in0=fn[:, p, :], scalar=ADD[p], in1=bank[:], op0=ALU.add, op1=ALU.mult
                )

        def plane_adds(t):
            fn, av = fns[t], avs[t + 1]
            for n in range(2):
                nc.gpsimd.tensor_tensor(out=av[:, n, :], in0=fn[:, 2 * n, :], in1=fn[:, 2 * n + 1, :], op=ALU.add)

        def adder(t, rows):
            fn = fns[t]
            if t + 1 < NTILES:
                av = avs[t + 1]
                planes = [fn[:, 4, :], fn[:, 5, :], av[:, 0, :], av[:, 1, :]]
            else:
                planes = [fn[:, a, :] for a in range(6)]
            if 0 in rows:
                obs[t] = aux.tile([P, 4, P], F32, tag="aux", name="ob")
            ob = obs[t]
            for r in rows:
                for n, plane in enumerate(planes):
                    nc.tensor.matmul(
                        out=ob[:, r, :],
                        lhsT=plane[:, P * r : P * r + P],
                        rhs=ident[:],
                        is_transpose=True,
                        start=(n == 0),
                        stop=(n == len(planes) - 1),
                    )

        def finish(t):
            j, bc = t // 4, t % 4
            ot = outp.tile([P, 4, P], F32, name="ot")
            nc.scalar.copy(out=ot[:], in_=obs[t][:])
            nc.sync.dma_start(
                out=out[512 * bc : 512 * bc + 512, P * j : P * j + P].rearrange("(r p) i -> p r i", p=P), in_=ot[:]
            )

        x_transpose(0)
        x_copy(0)
        g_transpose(0, 0)
        clamps(0)
        func_s(0, 0)
        g_copy(0, 0, True)
        g_transpose(0, 1)
        load_g(2)
        g_copy(0, 1, True)
        func_s(0, 1)
        g_quantise(0)
        func_s(0, 2)
        func_s(0, 3)
        w_regroup(0, 0, nc.vector.tensor_copy)
        w_quantise(0, 0)
        w_regroup(0, 1, nc.vector.tensor_copy)
        w_quantise(0, 1)
        x_transpose(1)
        x_copy(1)
        g_transpose(1, 0)
        g_copy(1, 0, False)
        g_transpose(1, 1)
        g_copy(1, 1, False)
        load_g(3)
        w_regroup(0, 2, nc.scalar.copy)
        load_w(2)
        for q in range(4):
            issue_mx(q)
        func_v(0, 1, 5)
        w_quantise(0, 2)
        base_regroup()
        for q in range(4, LEAD):
            issue_mx(q)
        x_transpose(2)
        x_transpose(3)
        x_copy(2)
        clamps(1)
        for t in range(NTILES):
            if t >= 1:
                plane_adds(t - 1)
            if t + 1 < NTILES:
                func_s(t + 1, 1)
                func_s(t + 1, 2)
            if t >= 2:
                finish(t - 2)
            if t + 1 < NTILES:
                func_s(t + 1, 3)
                func_s(t + 1, 0)
            if t + 3 < NTILES:
                x_copy(t + 3)
            jn, c = t // 4 + 1, t % 4
            weights = jn < 4 and c < 3
            if weights:
                w_regroup(jn, c, nc.scalar.copy)
            for n in range(NPLANES):
                q = NPLANES * t + n
                consume(q)
                if n in (1, 3) and t < 2:
                    g_transpose(t + 2, n // 2)
                    g_copy(t + 2, n // 2, False)
                if n == 2:
                    if t >= 1:
                        adder(t - 1, (0, 1, 2, 3))
                    if t + 4 < NTILES:
                        x_transpose(t + 4)
                if q == 1:
                    base_quantise()
                    issue_mx(LEAD)
                    g_quantise(1)
                if 0 < q < NPLANES * NTILES - LEAD:
                    issue_mx(q + LEAD)
            if t + 2 < NTILES:
                clamps(t + 2)
            if t + 1 < NTILES:
                func_v(t + 1, 1, 5)
            if t < 2:
                g_quantise(t + 2)
            if weights:
                w_quantise(jn, c)
            if t == 2:
                load_w(3)
        finish(NTILES - 2)
        adder(NTILES - 1, (0, 1, 2, 3))
        finish(NTILES - 1)
